import numpy as np
import ml_dtypes


def mxq(x, axis, fmt="e4m3"):
    dtype, down = {"e4m3": (ml_dtypes.float8_e4m3fn, 7), "e5m2": (ml_dtypes.float8_e5m2, 14)}[fmt]
    v = np.moveaxis(np.asarray(x, np.float32).astype(ml_dtypes.bfloat16).astype(np.float64), axis, -1)
    blocks = v.reshape(v.shape[:-1] + (-1, 32))
    amax = np.abs(blocks).max(-1, keepdims=True)
    byte = np.maximum(np.where(amax > 0, np.frexp(amax)[1] - 1 + 127, 0) - down, 1)
    scale = np.exp2(byte - 127.0)
    codes = (blocks / scale).astype(np.float32).astype(dtype).astype(np.float64)
    return np.moveaxis((codes * scale).reshape(v.shape), -1, axis)


WIDE = False


def mx_kscale(k):
    if not WIDE:
        return np.ones(k)
    levels = np.array([10, -10, 5, -5, 0])
    a = np.random.permutation(np.resize(levels, k // 512 * 4)).reshape(k // 512, 4)
    idx = np.arange(k)
    return np.exp2(a[idx // 512, idx % 128 // 32])


BF16 = ml_dtypes.bfloat16


def bf(x):
    return np.asarray(x, np.float32).astype(BF16)


def f64(x):
    return np.asarray(x).astype(np.float64)


B, N, DIM, R, KEY = 1, 1024, 1024, 4, 128
UV = DIM * R // 2
NORM_EPS = 1e-12


def silu(z):
    return z / (1.0 + np.exp(-z))


def setup_inputs():
    t = np.exp2(np.round(np.log2(mx_kscale(N)) / 2))
    r = mx_kscale(UV)
    return {"q": bf(np.random.standard_normal((B, N, KEY)) * 1.2),
            "k": bf(np.random.standard_normal((B, N, KEY)) * 1.2 * t[:, None]),
            "u": bf(silu(np.random.standard_normal((B, N, UV))) * r),
            "v": bf(silu(np.random.standard_normal((B, N, UV))) / (t * t)[:, None]),
            "hidden_states": bf(np.random.standard_normal((B, N, DIM))),
            "Wo": bf(np.random.standard_normal((UV, DIM)) * 3.0 / np.sqrt(UV) / r[:, None]),
            "bo": bf(np.random.standard_normal(DIM) * 0.1)}


def reference(q, k, u, v, hidden_states, Wo, bo):
    a = f64(q) @ f64(k).transpose(0, 2, 1) / np.sqrt(KEY)
    A = np.square(np.maximum(a, 0.0)) / N
    av = mxq(A, 2, "e4m3") @ mxq(f64(v), 1, "e4m3")
    g = f64(u) * av
    gau_out = (mxq(g, 2, "e4m3") @ mxq(f64(Wo), 0, "e4m3")) + f64(bo)
    o = f64(hidden_states) + gau_out
    variance = np.mean(np.square(o), axis=-1, keepdims=True)
    return o / np.sqrt(variance + NORM_EPS)

@@ -1,0 +1,279 @@
+from contextlib import ExitStack
+
+import concourse.mybir as mybir
+from concourse.masks import make_identity
+
+F32 = mybir.dt.float32
+BF16 = mybir.dt.bfloat16
+U32 = mybir.dt.uint32
+U8 = mybir.dt.uint8
+FP8X4 = mybir.dt.float8_e4m3fn_x4
+ACT = mybir.ActivationFunctionType
+ALU = mybir.AluOpType
+
+P = 128
+PACK = 4
+K_PASS = P * PACK
+
+TOKENS = 1024
+KEY = 128
+UV = 2048
+DIM = 1024
+NORM_EPS = 1e-12
+
+TOKEN_TILES = TOKENS // P
+HALF_TILES = TOKEN_TILES // 2
+HALF = TOKENS // 2
+KEY_PASSES = TOKENS // K_PASS
+UV_PASSES = UV // K_PASS
+DIM_HALVES = DIM // 512
+QUANT = PACK * 512
+
+FLOPS = 2 * TOKENS * TOKENS * KEY + 2 * 2 * TOKENS * TOKENS * UV
+
+
+def tile_gau_ae_pb_kernel(tc, q, k, u, v, hidden_states, Wo, bo, out):
+    nc = tc.nc
+    with ExitStack() as ctx:
+        keep = ctx.enter_context(tc.tile_pool(name="keep", bufs=1))
+        raw = ctx.enter_context(tc.tile_pool(name="raw", bufs=2))
+        stage = ctx.enter_context(tc.tile_pool(name="stage", bufs=2))
+        small = ctx.enter_context(tc.tile_pool(name="small", bufs=3))
+        psum = ctx.enter_context(tc.psum_pool(name="psum", bufs=2))
+
+        k_view = k.flatten_outer_dims().rearrange("(g p t) d -> p g (t d)", g=KEY_PASSES, p=P, t=PACK)
+        v_view = v.flatten_outer_dims().rearrange("(g p t) e -> g p t e", g=KEY_PASSES, p=P, t=PACK)
+        q_view = q.flatten_outer_dims().rearrange("(c p) d -> p c d", p=P)
+        u_view = u.flatten_outer_dims().rearrange("(c p) e -> p c e", p=P)
+        hid_view = hidden_states.flatten_outer_dims().rearrange("(c p) d -> p c d", p=P)
+        out_view = out.flatten_outer_dims().rearrange("(c p) d -> c p d", p=P)
+        wo_view = Wo.rearrange("(G h p e) d -> G p h (e d)", G=UV_PASSES, h=2, p=P, e=2)
+
+        ident_bf = keep.tile([P, P], BF16)
+        ident_f32 = keep.tile([P, P], F32)
+        kT = keep.tile([P, KEY_PASSES, PACK, P], BF16)
+        qT = keep.tile([P, TOKEN_TILES, P], BF16)
+        at_codes = keep.tile([P, KEY_PASSES, TOKENS], U32, align_bytes=64)
+        at_scales = keep.tile([P, KEY_PASSES, TOKENS], U8, align_bytes=64)
+        v_codes = keep.tile([P, KEY_PASSES, UV], U32, align_bytes=64)
+        v_scales = keep.tile([P, KEY_PASSES, UV], U8, align_bytes=64)
+        g_codes = keep.tile([P, UV_PASSES, TOKENS], U32, align_bytes=64)
+        g_scales = keep.tile([P, UV_PASSES, TOKENS], U8, align_bytes=64)
+        wo_codes = keep.tile([P, UV_PASSES, DIM], U32, align_bytes=64)
+        wo_scales = keep.tile([P, UV_PASSES, DIM], U8, align_bytes=64)
+        uT = keep.tile([P, UV_PASSES, TOKENS * 2], F32)
+        bo_all = keep.tile([P, DIM], BF16)
+        eps = keep.tile([P, 1], F32)
+        warm = keep.tile([P, 1], F32)
+        squares = keep.tile([P, DIM], BF16)
+
+        def load_v(G):
+            v_raw = raw.tile([P, KEY_PASSES, PACK, 512], BF16, tag="v_raw", name="v_raw")
+            for g in range(KEY_PASSES):
+                nc.sync.dma_start(out=v_raw[:, g, :, :], in_=v_view[g, :, :, G * 512 : (G + 1) * 512])
+            return v_raw
+
+        def load_hidden(half):
+            hid = raw.tile([P, HALF_TILES, DIM], BF16, tag="v_raw", name="hid")
+            nc.sync.dma_start(out=hid[:], in_=hid_view[:, half * HALF_TILES : (half + 1) * HALF_TILES, :])
+            return hid
+
+        def load_u(step):
+            half, G = divmod(step, UV_PASSES)
+            u_raw = raw.tile([P, HALF_TILES * 512], BF16, tag="u_raw", name="u_raw")
+            nc.sync.dma_start(
+                out=u_raw[:].rearrange("p (c e) -> p c e", c=HALF_TILES),
+                in_=u_view[:, half * HALF_TILES : (half + 1) * HALF_TILES, G * 512 : (G + 1) * 512],
+            )
+            return u_raw
+
+        def load_wo(G):
+            wo_raw = raw.tile([P, PACK, DIM], BF16, tag="wo_raw", name="wo_raw")
+            nc.sync.dma_start(out=wo_raw[:].rearrange("p (h e) d -> p h (e d)", h=2), in_=wo_view[G])
+            return wo_raw
+
+        def attention_weights(half, g):
+            relu = stage.tile([P, QUANT], F32, tag="relu", name="relu")
+            for cl in range(HALF_TILES):
+                c = half * HALF_TILES + cl
+                bank = psum.tile([P, PACK, P], F32, tag="quad", bufs=4, name="a_bank")
+                for t in range(PACK):
+                    nc.tensor.matmul(out=bank[:, t, :], lhsT=kT[:, g, t, :], rhs=qT[:, c, :], start=True, stop=True)
+                nc.scalar.activation(
+                    out=relu[:, cl * 512 : (cl + 1) * 512].rearrange("p (n t) -> p n t", t=PACK),
+                    in_=bank[:].rearrange("p t n -> p n t"),
+                    func=ACT.Relu,
+                )
+            at_grouped = stage.tile([P, QUANT], BF16, tag="at_grouped", name="at_grouped", align_bytes=64)
+            nc.scalar.activation(out=at_grouped[:], in_=relu[:], func=ACT.Square, scale=(KEY * TOKENS) ** -0.5)
+            cols = slice(half * HALF, (half + 1) * HALF)
+            nc.vector.quantize_mx(
+                out=at_codes[:, g, cols].bitcast(FP8X4), scales=at_scales[:, g, cols], in_=at_grouped[:]
+            )
+
+        def quantise_v(G, v_raw):
+            for g in range(KEY_PASSES):
+                v_grouped = stage.tile([P, QUANT], BF16, tag="grouped", bufs=3, name="v_grouped", align_bytes=64)
+                for h in range(2):
+                    nc.vector.tensor_copy(
+                        out=v_grouped[:, h * 1024 : (h + 1) * 1024].rearrange("p (e w t) -> p e w t", e=2, t=PACK),
+                        in_=v_raw[:, g, :, h * 256 : (h + 1) * 256].rearrange("p t (w e) -> p e w t", e=2),
+                    )
+                cols = slice(G * 512, (G + 1) * 512)
+                nc.vector.quantize_mx(
+                    out=v_codes[:, g, cols].bitcast(FP8X4), scales=v_scales[:, g, cols], in_=v_grouped[:]
+                )
+
+        def quantise_wo(G, wo_raw):
+            for dh in range(DIM_HALVES):
+                wo_grouped = stage.tile([P, QUANT], BF16, tag="grouped", bufs=3, name="wo_grouped", align_bytes=64)
+                dst = wo_grouped[:].rearrange("p (c i t) -> p c t i", i=4, t=PACK)
+                src = wo_raw[:, :, dh * 512 : (dh + 1) * 512].rearrange("p t (c i) -> p c t i", i=4)
+                if dh == 0:
+                    nc.vector.tensor_copy(out=dst, in_=src)
+                else:
+                    nc.scalar.copy(out=dst, in_=src)
+                cols = slice(dh * 512, (dh + 1) * 512)
+                nc.vector.quantize_mx(
+                    out=wo_codes[:, G, cols].bitcast(FP8X4), scales=wo_scales[:, G, cols], in_=wo_grouped[:]
+                )
+
+        def transpose_u(step, u_raw):
+            half, G = divmod(step, UV_PASSES)
+            words = u_raw[:].bitcast(F32)
+            for pair in range(HALF_TILES // 2):
+                bank = psum.tile([P, 2, 2 * P], F32, tag="tr", name="u_bank")
+                for c2 in range(2):
+                    for h in range(2):
+                        first = (2 * pair + c2) * 256 + h * P
+                        nc.tensor.transpose(bank[:, h, c2 * P : (c2 + 1) * P], words[:, first : first + P], ident_f32[:])
+                first = (half * HALF + pair * 2 * P) * 2
+                nc.scalar.copy(
+                    out=uT[:, G, first : first + 512].rearrange("p (n h) -> p n h", h=2),
+                    in_=bank[:].rearrange("p h n -> p n h"),
+                )
+
+        def values_passes(step):
+            half, G = divmod(step, UV_PASSES)
+            banks = []
+            for cl in range(HALF_TILES):
+                c = half * HALF_TILES + cl
+                bank = psum.tile([P, PACK, P], F32, tag="quad", bufs=4, name="av_bank")
+                for j in range(PACK):
+                    e_cols = slice(G * 512 + j * P, G * 512 + (j + 1) * P)
+                    n_cols = slice(c * P, (c + 1) * P)
+                    for g in range(KEY_PASSES):
+                        nc.tensor.matmul_mx(
+                            out=bank[:, j, :],
+                            lhsT=v_codes[:, g, e_cols].bitcast(FP8X4),
+                            lhsT_scale=v_scales[:, g, e_cols],
+                            rhs=at_codes[:, g, n_cols].bitcast(FP8X4),
+                            rhs_scale=at_scales[:, g, n_cols],
+                            start=(g == 0),
+                            stop=(g == KEY_PASSES - 1),
+                        )
+                banks.append(bank)
+            return banks
+
+        def gate(step, banks):
+            half, G = divmod(step, UV_PASSES)
+            g_grouped = stage.tile([P, QUANT], BF16, tag="g_grouped", name="g_grouped", align_bytes=64)
+            for cl in range(HALF_TILES):
+                c = half * HALF_TILES + cl
+                nc.vector.tensor_tensor(
+                    out=g_grouped[:, cl * 512 : (cl + 1) * 512].rearrange("p (n j) -> p n j", j=PACK),
+                    in0=banks[cl][:].rearrange("p j n -> p n j"),
+                    in1=uT[:, G, c * 256 : (c + 1) * 256].bitcast(BF16).rearrange("p (n j) -> p n j", j=PACK),
+                    op=ALU.mult,
+                )
+            cols = slice(half * HALF, (half + 1) * HALF)
+            nc.vector.quantize_mx(out=g_codes[:, G, cols].bitcast(FP8X4), scales=g_scales[:, G, cols], in_=g_grouped[:])
+
+        def output_tile(c, hid):
+            o = stage.tile([P, DIM], F32, tag="o", bufs=3, name="o")
+            nc.gpsimd.tensor_tensor(out=o[:], in0=hid[:, c % HALF_TILES, :], in1=bo_all[:], op=ALU.add)
+            n_cols = slice(c * P, (c + 1) * P)
+            for dh in range(DIM_HALVES):
+                d_cols = slice(dh * 512, (dh + 1) * 512)
+                bank = psum.tile([P, 512], F32, tag="wide", name="o_bank")
+                for G in range(UV_PASSES):
+                    nc.tensor.matmul_mx(
+                        out=bank[:],
+                        lhsT=g_codes[:, G, n_cols].bitcast(FP8X4),
+                        lhsT_scale=g_scales[:, G, n_cols],
+                        rhs=wo_codes[:, G, d_cols].bitcast(FP8X4),
+                        rhs_scale=wo_scales[:, G, d_cols],
+                        start=(G == 0),
+                        stop=(G == UV_PASSES - 1),
+                    )
+                nc.vector.tensor_tensor(out=o[:, d_cols], in0=bank[:], in1=o[:, d_cols], op=ALU.add)
+            sum_sq = small.tile([P, 1], F32, tag="sum_sq", name="sum_sq")
+            rms = small.tile([P, 1], F32, tag="rms", name="rms")
+            inv_rms = small.tile([P, 1], F32, tag="inv_rms", name="inv_rms")
+            nc.scalar.activation(out=squares[:], in_=o[:], func=ACT.Square, accum_out=sum_sq[:])
+            nc.scalar.activation(out=rms[:], in_=sum_sq[:], func=ACT.Sqrt, scale=1.0 / DIM, bias=eps[:])
+            nc.vector.reciprocal(out=inv_rms[:], in_=rms[:])
+            nc.scalar.activation(out=o[:], in_=o[:], func=ACT.Copy, scale=inv_rms[:])
+            nc.sync.dma_start(out=out_view[c], in_=o[:])
+
+        k_sb = keep.tile([P, KEY_PASSES, PACK * KEY], BF16)
+        q_sb = keep.tile([P, TOKEN_TILES, KEY], BF16)
+        nc.sync.dma_start(out=k_sb[:], in_=k_view)
+        nc.sync.dma_start(out=q_sb[:], in_=q_view)
+        nc.gpsimd.dma_start(out=bo_all[:], in_=bo.partition_broadcast(P))
+        v_tiles = {0: load_v(0)}
+        u_tiles = {0: load_u(0)}
+        v_tiles[1] = load_v(1)
+        u_tiles[1] = load_u(1)
+        wo_tiles = {0: load_wo(0), 1: load_wo(1)}
+        hid_tiles = {}
+
+        make_identity(nc, ident_bf[:])
+        make_identity(nc, ident_f32[:])
+        nc.vector.memset(eps[:], NORM_EPS)
+        nc.vector.memset(warm[:], 1.0)
+        nc.scalar.activation(out=warm[:], in_=warm[:], func=ACT.Sqrt)
+
+        for g in range(KEY_PASSES):
+            bank = psum.tile([P, PACK, P], BF16, tag="tr", name="k_bank")
+            for t in range(PACK):
+                nc.tensor.transpose(bank[:, t, :], k_sb[:, g, t * KEY : (t + 1) * KEY], ident_bf[:])
+            nc.vector.tensor_copy(out=kT[:, g, :, :], in_=bank[:])
+        for half in range(2):
+            bank = psum.tile([P, HALF_TILES, P], BF16, tag="tr", name="q_bank")
+            for cl in range(HALF_TILES):
+                nc.tensor.transpose(bank[:, cl, :], q_sb[:, half * HALF_TILES + cl, :], ident_bf[:])
+            nc.scalar.copy(out=qT[:, half * HALF_TILES : (half + 1) * HALF_TILES, :], in_=bank[:])
+
+        for g in range(KEY_PASSES):
+            attention_weights(0, g)
+        quantise_v(0, v_tiles[0])
+        v_tiles[2] = load_v(2)
+        transpose_u(0, u_tiles[0])
+        u_tiles[2] = load_u(2)
+
+        steps = 2 * UV_PASSES
+        for step in range(steps):
+            half, G = divmod(step, UV_PASSES)
+            banks = values_passes(step)
+            if step + 1 < UV_PASSES:
+                quantise_v(G + 1, v_tiles[G + 1])
+                if G + 3 < UV_PASSES:
+                    v_tiles[G + 3] = load_v(G + 3)
+                else:
+                    hid_tiles[G + 3 - UV_PASSES] = load_hidden(G + 3 - UV_PASSES)
+            if step + 1 < steps:
+                transpose_u(step + 1, u_tiles[step + 1])
+                if step + 3 < steps:
+                    u_tiles[step + 3] = load_u(step + 3)
+            if half == 0:
+                quantise_wo(G, wo_tiles[G])
+                if G + 2 < UV_PASSES:
+                    wo_tiles[G + 2] = load_wo(G + 2)
+            gate(step, banks)
+            if step in (1, 2):
+                attention_weights(1, step - 1)
+            if half == 1:
+                output_tile(G, hid_tiles[0])
+        for c in range(HALF_TILES, TOKEN_TILES):
+            output_tile(c, hid_tiles[1])

@@ -14,6 +14,7 @@ ALU = mybir.AluOpType
 P = 128
 PACK = 4
 K_PASS = P * PACK
+BANK = 512
 
 TOKENS = 1024
 KEY = 128
@@ -22,12 +23,12 @@ DIM = 1024
 NORM_EPS = 1e-12
 
 TOKEN_TILES = TOKENS // P
-HALF_TILES = TOKEN_TILES // 2
-HALF = TOKENS // 2
+GROUP_TILES = 2
+GROUP = GROUP_TILES * P
+GROUPS = TOKENS // GROUP
 KEY_PASSES = TOKENS // K_PASS
 UV_PASSES = UV // K_PASS
-DIM_HALVES = DIM // 512
-QUANT = PACK * 512
+DIM_HALVES = DIM // BANK
 
 FLOPS = 2 * TOKENS * TOKENS * KEY + 2 * 2 * TOKENS * TOKENS * UV
 
@@ -35,11 +36,12 @@ FLOPS = 2 * TOKENS * TOKENS * KEY + 2 * 2 * TOKENS * TOKENS * UV
 def tile_gau_ae_pb_kernel(tc, q, k, u, v, hidden_states, Wo, bo, out):
     nc = tc.nc
     with ExitStack() as ctx:
+        ctx.enter_context(tc.manual_schedule())
         keep = ctx.enter_context(tc.tile_pool(name="keep", bufs=1))
         raw = ctx.enter_context(tc.tile_pool(name="raw", bufs=2))
         stage = ctx.enter_context(tc.tile_pool(name="stage", bufs=2))
         small = ctx.enter_context(tc.tile_pool(name="small", bufs=3))
-        psum = ctx.enter_context(tc.psum_pool(name="psum", bufs=2))
+        psum = ctx.enter_context(tc.psum_pool(name="psum", bufs=4))
 
         k_view = k.flatten_outer_dims().rearrange("(g p t) d -> p g (t d)", g=KEY_PASSES, p=P, t=PACK)
         v_view = v.flatten_outer_dims().rearrange("(g p t) e -> g p t e", g=KEY_PASSES, p=P, t=PACK)
@@ -51,6 +53,8 @@ def tile_gau_ae_pb_kernel(tc, q, k, u, v, hidden_states, Wo, bo, out):
 
         ident_bf = keep.tile([P, P], BF16)
         ident_f32 = keep.tile([P, P], F32)
+        k_sb = keep.tile([P, KEY_PASSES, PACK * KEY], BF16)
+        q_sb = keep.tile([P, TOKEN_TILES, KEY], BF16)
         kT = keep.tile([P, KEY_PASSES, PACK, P], BF16)
         qT = keep.tile([P, TOKEN_TILES, P], BF16)
         at_codes = keep.tile([P, KEY_PASSES, TOKENS], U32, align_bytes=64)
@@ -68,22 +72,22 @@ def tile_gau_ae_pb_kernel(tc, q, k, u, v, hidden_states, Wo, bo, out):
         squares = keep.tile([P, DIM], BF16)
 
         def load_v(G):
-            v_raw = raw.tile([P, KEY_PASSES, PACK, 512], BF16, tag="v_raw", name="v_raw")
+            v_raw = raw.tile([P, KEY_PASSES, PACK, K_PASS], BF16, tag="v_raw", name="v_raw")
             for g in range(KEY_PASSES):
-                nc.sync.dma_start(out=v_raw[:, g, :, :], in_=v_view[g, :, :, G * 512 : (G + 1) * 512])
+                nc.sync.dma_start(out=v_raw[:, g, :, :], in_=v_view[g, :, :, G * K_PASS : (G + 1) * K_PASS])
             return v_raw
 
         def load_hidden(half):
-            hid = raw.tile([P, HALF_TILES, DIM], BF16, tag="v_raw", name="hid")
-            nc.sync.dma_start(out=hid[:], in_=hid_view[:, half * HALF_TILES : (half + 1) * HALF_TILES, :])
+            tiles = TOKEN_TILES // 2
+            hid = raw.tile([P, tiles, DIM], BF16, tag="v_raw", name="hid")
+            nc.sync.dma_start(out=hid[:], in_=hid_view[:, half * tiles : (half + 1) * tiles, :])
             return hid
 
-        def load_u(step):
-            half, G = divmod(step, UV_PASSES)
-            u_raw = raw.tile([P, HALF_TILES * 512], BF16, tag="u_raw", name="u_raw")
+        def load_u(tg):
+            u_raw = raw.tile([P, GROUP_TILES * UV], BF16, tag="u_raw", name="u_raw")
             nc.sync.dma_start(
-                out=u_raw[:].rearrange("p (c e) -> p c e", c=HALF_TILES),
-                in_=u_view[:, half * HALF_TILES : (half + 1) * HALF_TILES, G * 512 : (G + 1) * 512],
+                out=u_raw[:].rearrange("p (c e) -> p c e", c=GROUP_TILES),
+                in_=u_view[:, tg * GROUP_TILES : (tg + 1) * GROUP_TILES, :],
             )
             return u_raw
 
@@ -92,76 +96,80 @@ def tile_gau_ae_pb_kernel(tc, q, k, u, v, hidden_states, Wo, bo, out):
             nc.sync.dma_start(out=wo_raw[:].rearrange("p (h e) d -> p h (e d)", h=2), in_=wo_view[G])
             return wo_raw
 
-        def attention_weights(half, g):
-            relu = stage.tile([P, QUANT], F32, tag="relu", name="relu")
-            for cl in range(HALF_TILES):
-                c = half * HALF_TILES + cl
-                bank = psum.tile([P, PACK, P], F32, tag="quad", bufs=4, name="a_bank")
+        def attention_weights(tg, g):
+            relu = stage.tile([P, PACK * GROUP], F32, tag="relu", name="relu")
+            for cl in range(GROUP_TILES):
+                c = tg * GROUP_TILES + cl
+                bank = psum.tile([P, PACK, P], F32, tag="bank", name="a_bank")
                 for t in range(PACK):
                     nc.tensor.matmul(out=bank[:, t, :], lhsT=kT[:, g, t, :], rhs=qT[:, c, :], start=True, stop=True)
                 nc.scalar.activation(
-                    out=relu[:, cl * 512 : (cl + 1) * 512].rearrange("p (n t) -> p n t", t=PACK),
+                    out=relu[:, cl * BANK : (cl + 1) * BANK].rearrange("p (n t) -> p n t", t=PACK),
                     in_=bank[:].rearrange("p t n -> p n t"),
                     func=ACT.Relu,
                 )
-            at_grouped = stage.tile([P, QUANT], BF16, tag="at_grouped", name="at_grouped", align_bytes=64)
+            at_grouped = stage.tile([P, PACK * GROUP], BF16, tag="at_grouped", name="at_grouped", align_bytes=64)
             nc.scalar.activation(out=at_grouped[:], in_=relu[:], func=ACT.Square, scale=(KEY * TOKENS) ** -0.5)
-            cols = slice(half * HALF, (half + 1) * HALF)
+            return at_grouped
+
+        def quantise_attention_weights(tg, g, at_grouped):
+            cols = slice(tg * GROUP, (tg + 1) * GROUP)
             nc.vector.quantize_mx(
                 out=at_codes[:, g, cols].bitcast(FP8X4), scales=at_scales[:, g, cols], in_=at_grouped[:]
             )
 
         def quantise_v(G, v_raw):
+            grouped = []
             for g in range(KEY_PASSES):
-                v_grouped = stage.tile([P, QUANT], BF16, tag="grouped", bufs=3, name="v_grouped", align_bytes=64)
+                v_grouped = stage.tile([P, PACK * K_PASS], BF16, tag="by_vector", bufs=3, name="v_grouped", align_bytes=64)
                 for h in range(2):
                     nc.vector.tensor_copy(
                         out=v_grouped[:, h * 1024 : (h + 1) * 1024].rearrange("p (e w t) -> p e w t", e=2, t=PACK),
                         in_=v_raw[:, g, :, h * 256 : (h + 1) * 256].rearrange("p t (w e) -> p e w t", e=2),
                     )
-                cols = slice(G * 512, (G + 1) * 512)
+                grouped.append(v_grouped)
+            cols = slice(G * K_PASS, (G + 1) * K_PASS)
+            for g in range(KEY_PASSES):
                 nc.vector.quantize_mx(
-                    out=v_codes[:, g, cols].bitcast(FP8X4), scales=v_scales[:, g, cols], in_=v_grouped[:]
+                    out=v_codes[:, g, cols].bitcast(FP8X4), scales=v_scales[:, g, cols], in_=grouped[g][:]
                 )
 
-        def quantise_wo(G, wo_raw):
-            for dh in range(DIM_HALVES):
-                wo_grouped = stage.tile([P, QUANT], BF16, tag="grouped", bufs=3, name="wo_grouped", align_bytes=64)
-                dst = wo_grouped[:].rearrange("p (c i t) -> p c t i", i=4, t=PACK)
-                src = wo_raw[:, :, dh * 512 : (dh + 1) * 512].rearrange("p t (c i) -> p c t i", i=4)
-                if dh == 0:
-                    nc.vector.tensor_copy(out=dst, in_=src)
-                else:
-                    nc.scalar.copy(out=dst, in_=src)
-                cols = slice(dh * 512, (dh + 1) * 512)
-                nc.vector.quantize_mx(
-                    out=wo_codes[:, G, cols].bitcast(FP8X4), scales=wo_scales[:, G, cols], in_=wo_grouped[:]
-                )
+        def regroup_wo(engine_copy, tag, wo_raw, dh):
+            wo_grouped = stage.tile([P, PACK * BANK], BF16, tag=tag, bufs=3, name="wo_grouped", align_bytes=64)
+            engine_copy(
+                out=wo_grouped[:].rearrange("p (c i t) -> p c t i", i=4, t=PACK),
+                in_=wo_raw[:, :, dh * BANK : (dh + 1) * BANK].rearrange("p t (c i) -> p c t i", i=4),
+            )
+            return wo_grouped
 
-        def transpose_u(step, u_raw):
-            half, G = divmod(step, UV_PASSES)
+        def quantise_wo(G, dh, wo_grouped):
+            cols = slice(dh * BANK, (dh + 1) * BANK)
+            nc.vector.quantize_mx(
+                out=wo_codes[:, G, cols].bitcast(FP8X4), scales=wo_scales[:, G, cols], in_=wo_grouped[:]
+            )
+
+        def transpose_u(tg, u_raw):
             words = u_raw[:].bitcast(F32)
-            for pair in range(HALF_TILES // 2):
-                bank = psum.tile([P, 2, 2 * P], F32, tag="tr", name="u_bank")
-                for c2 in range(2):
+            for G in range(UV_PASSES):
+                bank = psum.tile([P, 2, GROUP], F32, tag="bank", name="u_bank")
+                for cl in range(GROUP_TILES):
                     for h in range(2):
-                        first = (2 * pair + c2) * 256 + h * P
-                        nc.tensor.transpose(bank[:, h, c2 * P : (c2 + 1) * P], words[:, first : first + P], ident_f32[:])
-                first = (half * HALF + pair * 2 * P) * 2
+                        first = cl * (UV // 2) + G * (K_PASS // 2) + h * P
+                        nc.tensor.transpose(bank[:, h, cl * P : (cl + 1) * P], words[:, first : first + P], ident_f32[:])
                 nc.scalar.copy(
-                    out=uT[:, G, first : first + 512].rearrange("p (n h) -> p n h", h=2),
+                    out=uT[:, G, tg * GROUP * 2 : (tg + 1) * GROUP * 2].rearrange("p (n h) -> p n h", h=2),
                     in_=bank[:].rearrange("p h n -> p n h"),
                 )
 
         def values_passes(step):
-            half, G = divmod(step, UV_PASSES)
+            tg, G = divmod(step, UV_PASSES)
             banks = []
-            for cl in range(HALF_TILES):
-                c = half * HALF_TILES + cl
-                bank = psum.tile([P, PACK, P], F32, tag="quad", bufs=4, name="av_bank")
+            for cl in range(GROUP_TILES):
+                c = tg * GROUP_TILES + cl
+                n_cols = slice(c * P, (c + 1) * P)
+                bank = psum.tile([P, PACK, P], F32, tag="bank", name="av_bank")
                 for j in range(PACK):
-                    e_cols = slice(G * 512 + j * P, G * 512 + (j + 1) * P)
-                    n_cols = slice(c * P, (c + 1) * P)
+                    e_cols = slice(G * K_PASS + j * P, G * K_PASS + (j + 1) * P)
                     for g in range(KEY_PASSES):
                         nc.tensor.matmul_mx(
                             out=bank[:, j, :],
@@ -176,29 +184,28 @@ def tile_gau_ae_pb_kernel(tc, q, k, u, v, hidden_states, Wo, bo, out):
             return banks
 
         def gate(step, banks):
-            half, G = divmod(step, UV_PASSES)
-            g_grouped = stage.tile([P, QUANT], BF16, tag="g_grouped", name="g_grouped", align_bytes=64)
-            for cl in range(HALF_TILES):
-                c = half * HALF_TILES + cl
+            tg, G = divmod(step, UV_PASSES)
+            g_grouped = stage.tile([P, PACK * GROUP], BF16, tag="g_grouped", name="g_grouped", align_bytes=64)
+            for cl in range(GROUP_TILES):
+                c = tg * GROUP_TILES + cl
                 nc.vector.tensor_tensor(
-                    out=g_grouped[:, cl * 512 : (cl + 1) * 512].rearrange("p (n j) -> p n j", j=PACK),
+                    out=g_grouped[:, cl * BANK : (cl + 1) * BANK].rearrange("p (n j) -> p n j", j=PACK),
                     in0=banks[cl][:].rearrange("p j n -> p n j"),
-                    in1=uT[:, G, c * 256 : (c + 1) * 256].bitcast(BF16).rearrange("p (n j) -> p n j", j=PACK),
+                    in1=uT[:, G, c * P * 2 : (c + 1) * P * 2].bitcast(BF16).rearrange("p (n j) -> p n j", j=PACK),
                     op=ALU.mult,
                 )
-            cols = slice(half * HALF, (half + 1) * HALF)
+            cols = slice(tg * GROUP, (tg + 1) * GROUP)
             nc.vector.quantize_mx(out=g_codes[:, G, cols].bitcast(FP8X4), scales=g_scales[:, G, cols], in_=g_grouped[:])
 
-        def output_tile(c, hid):
-            o = stage.tile([P, DIM], F32, tag="o", bufs=3, name="o")
-            nc.gpsimd.tensor_tensor(out=o[:], in0=hid[:, c % HALF_TILES, :], in1=bo_all[:], op=ALU.add)
-            n_cols = slice(c * P, (c + 1) * P)
-            for dh in range(DIM_HALVES):
-                d_cols = slice(dh * 512, (dh + 1) * 512)
-                bank = psum.tile([P, 512], F32, tag="wide", name="o_bank")
-                for G in range(UV_PASSES):
+        def output_passes(step, o_banks):
+            tg, G = divmod(step, UV_PASSES)
+            for cl in range(GROUP_TILES):
+                c = tg * GROUP_TILES + cl
+                n_cols = slice(c * P, (c + 1) * P)
+                for dh in range(DIM_HALVES):
+                    d_cols = slice(dh * BANK, (dh + 1) * BANK)
                     nc.tensor.matmul_mx(
-                        out=bank[:],
+                        out=o_banks[cl * DIM_HALVES + dh][:],
                         lhsT=g_codes[:, G, n_cols].bitcast(FP8X4),
                         lhsT_scale=g_scales[:, G, n_cols],
                         rhs=wo_codes[:, G, d_cols].bitcast(FP8X4),
@@ -206,74 +213,118 @@ def tile_gau_ae_pb_kernel(tc, q, k, u, v, hidden_states, Wo, bo, out):
                         start=(G == 0),
                         stop=(G == UV_PASSES - 1),
                     )
-                nc.vector.tensor_tensor(out=o[:, d_cols], in0=bank[:], in1=o[:, d_cols], op=ALU.add)
+
+        def residual_and_bias(c, hid):
+            o = stage.tile([P, DIM], F32, tag="o", bufs=4, name="o")
+            nc.gpsimd.tensor_tensor(out=o[:], in0=hid[:, c % (TOKEN_TILES // 2), :], in1=bo_all[:], op=ALU.add)
+            return o
+
+        def add_output(o, o_banks, cl):
+            for dh in range(DIM_HALVES):
+                d_cols = slice(dh * BANK, (dh + 1) * BANK)
+                nc.vector.tensor_tensor(out=o[:, d_cols], in0=o_banks[cl * DIM_HALVES + dh][:], in1=o[:, d_cols], op=ALU.add)
+
+        def norm_and_store(c, o):
             sum_sq = small.tile([P, 1], F32, tag="sum_sq", name="sum_sq")
-            rms = small.tile([P, 1], F32, tag="rms", name="rms")
             inv_rms = small.tile([P, 1], F32, tag="inv_rms", name="inv_rms")
             nc.scalar.activation(out=squares[:], in_=o[:], func=ACT.Square, accum_out=sum_sq[:])
-            nc.scalar.activation(out=rms[:], in_=sum_sq[:], func=ACT.Sqrt, scale=1.0 / DIM, bias=eps[:])
-            nc.vector.reciprocal(out=inv_rms[:], in_=rms[:])
-            nc.scalar.activation(out=o[:], in_=o[:], func=ACT.Copy, scale=inv_rms[:])
+            nc.scalar.activation(out=inv_rms[:], in_=sum_sq[:], func=ACT.Abs_reciprocal_sqrt, scale=1.0 / DIM, bias=eps[:])
+            nc.gpsimd.tensor_scalar(out=o[:], in0=o[:], scalar1=inv_rms[:], scalar2=0.0, op0=ALU.mult, op1=ALU.add)
             nc.sync.dma_start(out=out_view[c], in_=o[:])
 
-        k_sb = keep.tile([P, KEY_PASSES, PACK * KEY], BF16)
-        q_sb = keep.tile([P, TOKEN_TILES, KEY], BF16)
         nc.sync.dma_start(out=k_sb[:], in_=k_view)
         nc.sync.dma_start(out=q_sb[:], in_=q_view)
         nc.gpsimd.dma_start(out=bo_all[:], in_=bo.partition_broadcast(P))
         v_tiles = {0: load_v(0)}
         u_tiles = {0: load_u(0)}
         v_tiles[1] = load_v(1)
+        wo_tiles = {0: load_wo(0)}
         u_tiles[1] = load_u(1)
-        wo_tiles = {0: load_wo(0), 1: load_wo(1)}
+        wo_tiles[1] = load_wo(1)
         hid_tiles = {}
 
         make_identity(nc, ident_bf[:])
         make_identity(nc, ident_f32[:])
         nc.vector.memset(eps[:], NORM_EPS)
         nc.vector.memset(warm[:], 1.0)
-        nc.scalar.activation(out=warm[:], in_=warm[:], func=ACT.Sqrt)
+        nc.scalar.activation(out=warm[:], in_=warm[:], func=ACT.Abs_reciprocal_sqrt)
 
         for g in range(KEY_PASSES):
-            bank = psum.tile([P, PACK, P], BF16, tag="tr", name="k_bank")
+            bank = psum.tile([P, PACK, P], BF16, tag="bank", name="k_bank")
             for t in range(PACK):
                 nc.tensor.transpose(bank[:, t, :], k_sb[:, g, t * KEY : (t + 1) * KEY], ident_bf[:])
             nc.vector.tensor_copy(out=kT[:, g, :, :], in_=bank[:])
         for half in range(2):
-            bank = psum.tile([P, HALF_TILES, P], BF16, tag="tr", name="q_bank")
-            for cl in range(HALF_TILES):
-                nc.tensor.transpose(bank[:, cl, :], q_sb[:, half * HALF_TILES + cl, :], ident_bf[:])
-            nc.scalar.copy(out=qT[:, half * HALF_TILES : (half + 1) * HALF_TILES, :], in_=bank[:])
+            tiles = TOKEN_TILES // 2
+            bank = psum.tile([P, tiles, P], BF16, tag="bank", name="q_bank")
+            for cl in range(tiles):
+                nc.tensor.transpose(bank[:, cl, :], q_sb[:, half * tiles + cl, :], ident_bf[:])
+            nc.scalar.copy(out=qT[:, half * tiles : (half + 1) * tiles, :], in_=bank[:])
 
+        at_tiles = {}
         for g in range(KEY_PASSES):
-            attention_weights(0, g)
+            at_tiles[g] = attention_weights(0, g)
         quantise_v(0, v_tiles[0])
         v_tiles[2] = load_v(2)
+        for g in range(KEY_PASSES):
+            quantise_attention_weights(0, g, at_tiles[g])
         transpose_u(0, u_tiles[0])
         u_tiles[2] = load_u(2)
 
-        steps = 2 * UV_PASSES
+        steps = GROUPS * UV_PASSES
+        av_banks = values_passes(0)
+        o_tiles = {}
+        o_banks = {}
         for step in range(steps):
-            half, G = divmod(step, UV_PASSES)
-            banks = values_passes(step)
-            if step + 1 < UV_PASSES:
-                quantise_v(G + 1, v_tiles[G + 1])
-                if G + 3 < UV_PASSES:
-                    v_tiles[G + 3] = load_v(G + 3)
-                else:
-                    hid_tiles[G + 3 - UV_PASSES] = load_hidden(G + 3 - UV_PASSES)
-            if step + 1 < steps:
-                transpose_u(step + 1, u_tiles[step + 1])
-                if step + 3 < steps:
-                    u_tiles[step + 3] = load_u(step + 3)
-            if half == 0:
-                quantise_wo(G, wo_tiles[G])
+            tg, G = divmod(step, UV_PASSES)
+            if tg == 0:
+                if G == 0:
+                    for g in range(KEY_PASSES):
+                        at_tiles[g] = attention_weights(1, g)
+                by_scalar = regroup_wo(nc.scalar.copy, "by_scalar", wo_tiles[G], 1)
+                if G + 1 < GROUPS:
+                    transpose_u(G + 1, u_tiles[G + 1])
+                    if G + 3 < GROUPS:
+                        u_tiles[G + 3] = load_u(G + 3)
+                if G + 1 < UV_PASSES:
+                    quantise_v(G + 1, v_tiles[G + 1])
+                    if G + 3 < UV_PASSES:
+                        v_tiles[G + 3] = load_v(G + 3)
+                    else:
+                        hid_tiles[G + 3 - UV_PASSES] = load_hidden(G + 3 - UV_PASSES)
+                by_vector = regroup_wo(nc.vector.tensor_copy, "by_vector", wo_tiles[G], 0)
+                gate(step, av_banks)
+                quantise_wo(G, 0, by_vector)
+                if G == 0:
+                    for g in range(KEY_PASSES):
+                        quantise_attention_weights(1, g, at_tiles[g])
+                quantise_wo(G, 1, by_scalar)
                 if G + 2 < UV_PASSES:
                     wo_tiles[G + 2] = load_wo(G + 2)
-            gate(step, banks)
-            if step in (1, 2):
-                attention_weights(1, step - 1)
-            if half == 1:
-                output_tile(G, hid_tiles[0])
-        for c in range(HALF_TILES, TOKEN_TILES):
-            output_tile(c, hid_tiles[1])
+            else:
+                if tg + 1 < GROUPS and G < KEY_PASSES:
+                    at_tiles[G] = attention_weights(tg + 1, G)
+                gate(step, av_banks)
+                if G == 0:
+                    for cl in range(GROUP_TILES):
+                        add_output(o_tiles[(tg - 1) * GROUP_TILES + cl], o_banks[tg - 1], cl)
+                if G < GROUP_TILES:
+                    c = (tg - 1) * GROUP_TILES + G
+                    norm_and_store(c, o_tiles[c])
+                if tg + 1 < GROUPS and G >= KEY_PASSES:
+                    quantise_attention_weights(tg + 1, G - KEY_PASSES, at_tiles[G - KEY_PASSES])
+            if G == 2:
+                for cl in range(GROUP_TILES):
+                    c = tg * GROUP_TILES + cl
+                    o_tiles[c] = residual_and_bias(c, hid_tiles[c // (TOKEN_TILES // 2)])
+            if step + 1 < steps:
+                av_banks = values_passes(step + 1)
+            if G == 0:
+                o_banks[tg] = [
+                    psum.tile([P, BANK], F32, tag="wide", name="o_bank%d" % i) for i in range(GROUP_TILES * DIM_HALVES)
+                ]
+            output_passes(step, o_banks[tg])
+        for cl in range(GROUP_TILES):
+            c = (GROUPS - 1) * GROUP_TILES + cl
+            add_output(o_tiles[c], o_banks[GROUPS - 1], cl)
+            norm_and_store(c, o_tiles[c])

@@ -216,7 +216,7 @@ def tile_gau_ae_pb_kernel(tc, q, k, u, v, hidden_states, Wo, bo, out):
 
         def residual_and_bias(c, hid):
             o = stage.tile([P, DIM], F32, tag="o", bufs=4, name="o")
-            nc.gpsimd.tensor_tensor(out=o[:], in0=hid[:, c % (TOKEN_TILES // 2), :], in1=bo_all[:], op=ALU.add)
+            nc.vector.tensor_tensor(out=o[:], in0=hid[:, c % (TOKEN_TILES // 2), :], in1=bo_all[:], op=ALU.add)
             return o
 
         def add_output(o, o_banks, cl):
@@ -229,7 +229,7 @@ def tile_gau_ae_pb_kernel(tc, q, k, u, v, hidden_states, Wo, bo, out):
             inv_rms = small.tile([P, 1], F32, tag="inv_rms", name="inv_rms")
             nc.scalar.activation(out=squares[:], in_=o[:], func=ACT.Square, accum_out=sum_sq[:])
             nc.scalar.activation(out=inv_rms[:], in_=sum_sq[:], func=ACT.Abs_reciprocal_sqrt, scale=1.0 / DIM, bias=eps[:])
-            nc.gpsimd.tensor_scalar(out=o[:], in0=o[:], scalar1=inv_rms[:], scalar2=0.0, op0=ALU.mult, op1=ALU.add)
+            nc.scalar.activation(out=o[:], in_=o[:], func=ACT.Copy, scale=inv_rms[:])
             nc.sync.dma_start(out=out_view[c], in_=o[:])
 
         nc.sync.dma_start(out=k_sb[:], in_=k_view)

@@ -36,7 +36,6 @@ FLOPS = 2 * TOKENS * TOKENS * KEY + 2 * 2 * TOKENS * TOKENS * UV
 def tile_gau_ae_pb_kernel(tc, q, k, u, v, hidden_states, Wo, bo, out):
     nc = tc.nc
     with ExitStack() as ctx:
-        ctx.enter_context(tc.manual_schedule())
         keep = ctx.enter_context(tc.tile_pool(name="keep", bufs=1))
         raw = ctx.enter_context(tc.tile_pool(name="raw", bufs=2))
         stage = ctx.enter_context(tc.tile_pool(name="stage", bufs=2))

@@ -22,13 +22,12 @@ UV = 2048
 DIM = 1024
 NORM_EPS = 1e-12
 
-TOKEN_TILES = TOKENS // P
-GROUP_TILES = 2
-GROUP = GROUP_TILES * P
-GROUPS = TOKENS // GROUP
+TILES = TOKENS // P
 KEY_PASSES = TOKENS // K_PASS
 UV_PASSES = UV // K_PASS
+PAIRS = UV_PASSES // 2
 DIM_HALVES = DIM // BANK
+AHEAD = UV_PASSES
 
 FLOPS = 2 * TOKENS * TOKENS * KEY + 2 * 2 * TOKENS * TOKENS * UV
 
@@ -40,7 +39,7 @@ def tile_gau_ae_pb_kernel(tc, q, k, u, v, hidden_states, Wo, bo, out):
         raw = ctx.enter_context(tc.tile_pool(name="raw", bufs=2))
         stage = ctx.enter_context(tc.tile_pool(name="stage", bufs=2))
         small = ctx.enter_context(tc.tile_pool(name="small", bufs=3))
-        psum = ctx.enter_context(tc.psum_pool(name="psum", bufs=4))
+        psum = ctx.enter_context(tc.psum_pool(name="psum", bufs=2))
 
         k_view = k.flatten_outer_dims().rearrange("(g p t) d -> p g (t d)", g=KEY_PASSES, p=P, t=PACK)
         v_view = v.flatten_outer_dims().rearrange("(g p t) e -> g p t e", g=KEY_PASSES, p=P, t=PACK)
@@ -53,88 +52,75 @@ def tile_gau_ae_pb_kernel(tc, q, k, u, v, hidden_states, Wo, bo, out):
         ident_bf = keep.tile([P, P], BF16)
         ident_f32 = keep.tile([P, P], F32)
         k_sb = keep.tile([P, KEY_PASSES, PACK * KEY], BF16)
-        q_sb = keep.tile([P, TOKEN_TILES, KEY], BF16)
+        q_sb = keep.tile([P, TILES, KEY], BF16)
         kT = keep.tile([P, KEY_PASSES, PACK, P], BF16)
-        qT = keep.tile([P, TOKEN_TILES, P], BF16)
-        at_codes = keep.tile([P, KEY_PASSES, TOKENS], U32, align_bytes=64)
-        at_scales = keep.tile([P, KEY_PASSES, TOKENS], U8, align_bytes=64)
+        qT = keep.tile([P, TILES, P], BF16)
+        at_codes = keep.tile([P, TILES, KEY_PASSES * P], U32, align_bytes=64)
+        at_scales = keep.tile([P, TILES, KEY_PASSES * P], U8, align_bytes=64)
+        g_codes = keep.tile([P, TILES, UV_PASSES * P], U32, align_bytes=64)
+        g_scales = keep.tile([P, TILES, UV_PASSES * P], U8, align_bytes=64)
         v_codes = keep.tile([P, KEY_PASSES, UV], U32, align_bytes=64)
         v_scales = keep.tile([P, KEY_PASSES, UV], U8, align_bytes=64)
-        g_codes = keep.tile([P, UV_PASSES, TOKENS], U32, align_bytes=64)
-        g_scales = keep.tile([P, UV_PASSES, TOKENS], U8, align_bytes=64)
         wo_codes = keep.tile([P, UV_PASSES, DIM], U32, align_bytes=64)
         wo_scales = keep.tile([P, UV_PASSES, DIM], U8, align_bytes=64)
-        uT = keep.tile([P, UV_PASSES, TOKENS * 2], F32)
         bo_all = keep.tile([P, DIM], BF16)
         eps = keep.tile([P, 1], F32)
         warm = keep.tile([P, 1], F32)
         squares = keep.tile([P, DIM], BF16)
 
-        def load_v(G):
-            v_raw = raw.tile([P, KEY_PASSES, PACK, K_PASS], BF16, tag="v_raw", name="v_raw")
-            for g in range(KEY_PASSES):
-                nc.sync.dma_start(out=v_raw[:, g, :, :], in_=v_view[g, :, :, G * K_PASS : (G + 1) * K_PASS])
+        def load_v(G, g):
+            v_raw = raw.tile([P, PACK, K_PASS], BF16, tag="v_raw", bufs=8, name="v_raw")
+            nc.sync.dma_start(out=v_raw[:], in_=v_view[g, :, :, G * K_PASS : (G + 1) * K_PASS])
             return v_raw
 
-        def load_hidden(half):
-            tiles = TOKEN_TILES // 2
-            hid = raw.tile([P, tiles, DIM], BF16, tag="v_raw", name="hid")
-            nc.sync.dma_start(out=hid[:], in_=hid_view[:, half * tiles : (half + 1) * tiles, :])
+        def load_hidden(part):
+            hid = raw.tile([P, 2, DIM], BF16, tag="hid", bufs=2, name="hid")
+            nc.sync.dma_start(out=hid[:], in_=hid_view[:, part * 2 : (part + 1) * 2, :])
             return hid
 
-        def load_u(tg):
-            u_raw = raw.tile([P, GROUP_TILES * UV], BF16, tag="u_raw", name="u_raw")
-            nc.sync.dma_start(
-                out=u_raw[:].rearrange("p (c e) -> p c e", c=GROUP_TILES),
-                in_=u_view[:, tg * GROUP_TILES : (tg + 1) * GROUP_TILES, :],
-            )
+        def load_u(c):
+            u_raw = raw.tile([P, UV], BF16, tag="u_raw", bufs=3, name="u_raw")
+            nc.sync.dma_start(out=u_raw[:], in_=u_view[:, c, :])
             return u_raw
 
         def load_wo(G):
-            wo_raw = raw.tile([P, PACK, DIM], BF16, tag="wo_raw", name="wo_raw")
+            wo_raw = raw.tile([P, PACK, DIM], BF16, tag="wo_raw", bufs=2, name="wo_raw")
             nc.sync.dma_start(out=wo_raw[:].rearrange("p (h e) d -> p h (e d)", h=2), in_=wo_view[G])
             return wo_raw
 
-        def attention_weights(tg, g):
-            relu = stage.tile([P, PACK * GROUP], F32, tag="relu", name="relu")
-            for cl in range(GROUP_TILES):
-                c = tg * GROUP_TILES + cl
-                bank = psum.tile([P, PACK, P], F32, tag="bank", name="a_bank")
+        def attention_weights(c):
+            relu = stage.tile([P, KEY_PASSES * BANK], F32, tag="relu", bufs=2, name="relu")
+            for g in range(KEY_PASSES):
+                bank = psum.tile([P, PACK, P], F32, tag="bank", bufs=2, name="a_bank")
                 for t in range(PACK):
                     nc.tensor.matmul(out=bank[:, t, :], lhsT=kT[:, g, t, :], rhs=qT[:, c, :], start=True, stop=True)
                 nc.scalar.activation(
-                    out=relu[:, cl * BANK : (cl + 1) * BANK].rearrange("p (n t) -> p n t", t=PACK),
+                    out=relu[:, g * BANK : (g + 1) * BANK].rearrange("p (n t) -> p n t", t=PACK),
                     in_=bank[:].rearrange("p t n -> p n t"),
                     func=ACT.Relu,
                 )
-            at_grouped = stage.tile([P, PACK * GROUP], BF16, tag="at_grouped", name="at_grouped", align_bytes=64)
+            at_grouped = stage.tile([P, KEY_PASSES * BANK], BF16, tag="at_grouped", bufs=3, name="at_grouped", align_bytes=64)
             nc.scalar.activation(out=at_grouped[:], in_=relu[:], func=ACT.Square, scale=(KEY * TOKENS) ** -0.5)
             return at_grouped
 
-        def quantise_attention_weights(tg, g, at_grouped):
-            cols = slice(tg * GROUP, (tg + 1) * GROUP)
-            nc.vector.quantize_mx(
-                out=at_codes[:, g, cols].bitcast(FP8X4), scales=at_scales[:, g, cols], in_=at_grouped[:]
-            )
+        def quantise_attention_weights(c, at_grouped):
+            nc.vector.quantize_mx(out=at_codes[:, c, :].bitcast(FP8X4), scales=at_scales[:, c, :], in_=at_grouped[:])
 
-        def quantise_v(G, v_raw):
-            grouped = []
-            for g in range(KEY_PASSES):
-                v_grouped = stage.tile([P, PACK * K_PASS], BF16, tag="by_vector", bufs=3, name="v_grouped", align_bytes=64)
-                for h in range(2):
-                    nc.vector.tensor_copy(
-                        out=v_grouped[:, h * 1024 : (h + 1) * 1024].rearrange("p (e w t) -> p e w t", e=2, t=PACK),
-                        in_=v_raw[:, g, :, h * 256 : (h + 1) * 256].rearrange("p t (w e) -> p e w t", e=2),
-                    )
-                grouped.append(v_grouped)
-            cols = slice(G * K_PASS, (G + 1) * K_PASS)
-            for g in range(KEY_PASSES):
-                nc.vector.quantize_mx(
-                    out=v_codes[:, g, cols].bitcast(FP8X4), scales=v_scales[:, g, cols], in_=grouped[g][:]
+        def regroup_v(v_raw):
+            v_grouped = stage.tile([P, PACK * K_PASS], BF16, tag="v_grouped", bufs=3, name="v_grouped", align_bytes=64)
+            for h in range(2):
+                nc.vector.tensor_copy(
+                    out=v_grouped[:, h * 1024 : (h + 1) * 1024].rearrange("p (e w t) -> p e w t", e=2, t=PACK),
+                    in_=v_raw[:, :, h * 256 : (h + 1) * 256].rearrange("p t (w e) -> p e w t", e=2),
                 )
+            return v_grouped
 
-        def regroup_wo(engine_copy, tag, wo_raw, dh):
-            wo_grouped = stage.tile([P, PACK * BANK], BF16, tag=tag, bufs=3, name="wo_grouped", align_bytes=64)
+        def quantise_v(G, g, v_grouped):
+            cols = slice(G * K_PASS, (G + 1) * K_PASS)
+            nc.vector.quantize_mx(out=v_codes[:, g, cols].bitcast(FP8X4), scales=v_scales[:, g, cols], in_=v_grouped[:])
+
+        def regroup_wo(engine_copy, wo_raw, dh):
+            wo_grouped = stage.tile([P, PACK * BANK], BF16, tag="wo_grouped", bufs=3, name="wo_grouped", align_bytes=64)
             engine_copy(
                 out=wo_grouped[:].rearrange("p (c i t) -> p c t i", i=4, t=PACK),
                 in_=wo_raw[:, :, dh * BANK : (dh + 1) * BANK].rearrange("p t (c i) -> p c t i", i=4),
@@ -143,104 +129,114 @@ def tile_gau_ae_pb_kernel(tc, q, k, u, v, hidden_states, Wo, bo, out):
 
         def quantise_wo(G, dh, wo_grouped):
             cols = slice(dh * BANK, (dh + 1) * BANK)
-            nc.vector.quantize_mx(
-                out=wo_codes[:, G, cols].bitcast(FP8X4), scales=wo_scales[:, G, cols], in_=wo_grouped[:]
-            )
+            nc.vector.quantize_mx(out=wo_codes[:, G, cols].bitcast(FP8X4), scales=wo_scales[:, G, cols], in_=wo_grouped[:])
 
-        def transpose_u(tg, u_raw):
+        def transpose_u(c, u_raw):
+            uT = stage.tile([P, UV_PASSES, P * 2], F32, tag="uT", bufs=5, name="uT")
             words = u_raw[:].bitcast(F32)
-            for G in range(UV_PASSES):
-                bank = psum.tile([P, 2, GROUP], F32, tag="bank", name="u_bank")
-                for cl in range(GROUP_TILES):
+            for pair in range(PAIRS):
+                bank = psum.tile([P, 2, 2, P], F32, tag="bank", bufs=2, name="u_bank")
+                for i in range(2):
                     for h in range(2):
-                        first = cl * (UV // 2) + G * (K_PASS // 2) + h * P
-                        nc.tensor.transpose(bank[:, h, cl * P : (cl + 1) * P], words[:, first : first + P], ident_f32[:])
+                        first = ((2 * pair + i) * 2 + h) * P
+                        nc.tensor.transpose(bank[:, i, h, :], words[:, first : first + P], ident_f32[:])
                 nc.scalar.copy(
-                    out=uT[:, G, tg * GROUP * 2 : (tg + 1) * GROUP * 2].rearrange("p (n h) -> p n h", h=2),
-                    in_=bank[:].rearrange("p h n -> p n h"),
+                    out=uT[:, 2 * pair : 2 * pair + 2, :].rearrange("p i (n h) -> p i n h", h=2),
+                    in_=bank[:].rearrange("p i h n -> p i n h"),
                 )
+            return uT
 
-        def values_passes(step):
-            tg, G = divmod(step, UV_PASSES)
+        def values_passes(c, pair):
             banks = []
-            for cl in range(GROUP_TILES):
-                c = tg * GROUP_TILES + cl
-                n_cols = slice(c * P, (c + 1) * P)
-                bank = psum.tile([P, PACK, P], F32, tag="bank", name="av_bank")
+            for i in range(2):
+                G = 2 * pair + i
+                bank = psum.tile([P, PACK, P], F32, tag="wide", bufs=6, name="av_bank")
                 for j in range(PACK):
                     e_cols = slice(G * K_PASS + j * P, G * K_PASS + (j + 1) * P)
                     for g in range(KEY_PASSES):
+                        n_cols = slice(g * P, (g + 1) * P)
                         nc.tensor.matmul_mx(
                             out=bank[:, j, :],
                             lhsT=v_codes[:, g, e_cols].bitcast(FP8X4),
                             lhsT_scale=v_scales[:, g, e_cols],
-                            rhs=at_codes[:, g, n_cols].bitcast(FP8X4),
-                            rhs_scale=at_scales[:, g, n_cols],
+                            rhs=at_codes[:, c, n_cols].bitcast(FP8X4),
+                            rhs_scale=at_scales[:, c, n_cols],
                             start=(g == 0),
                             stop=(g == KEY_PASSES - 1),
                         )
                 banks.append(bank)
             return banks
 
-        def gate(step, banks):
-            tg, G = divmod(step, UV_PASSES)
-            g_grouped = stage.tile([P, PACK * GROUP], BF16, tag="g_grouped", name="g_grouped", align_bytes=64)
-            for cl in range(GROUP_TILES):
-                c = tg * GROUP_TILES + cl
+        def gate(uT, pair, banks):
+            g_grouped = stage.tile([P, 2, BANK], BF16, tag="g_grouped", bufs=3, name="g_grouped", align_bytes=64)
+            for i in range(2):
                 nc.vector.tensor_tensor(
-                    out=g_grouped[:, cl * BANK : (cl + 1) * BANK].rearrange("p (n j) -> p n j", j=PACK),
-                    in0=banks[cl][:].rearrange("p j n -> p n j"),
-                    in1=uT[:, G, c * P * 2 : (c + 1) * P * 2].bitcast(BF16).rearrange("p (n j) -> p n j", j=PACK),
+                    out=g_grouped[:, i, :].rearrange("p (n j) -> p n j", j=PACK),
+                    in0=banks[i][:].rearrange("p j n -> p n j"),
+                    in1=uT[:, 2 * pair + i, :].bitcast(BF16).rearrange("p (n j) -> p n j", j=PACK),
                     op=ALU.mult,
                 )
-            cols = slice(tg * GROUP, (tg + 1) * GROUP)
-            nc.vector.quantize_mx(out=g_codes[:, G, cols].bitcast(FP8X4), scales=g_scales[:, G, cols], in_=g_grouped[:])
+            return g_grouped
 
-        def output_passes(step, o_banks):
-            tg, G = divmod(step, UV_PASSES)
-            for cl in range(GROUP_TILES):
-                c = tg * GROUP_TILES + cl
-                n_cols = slice(c * P, (c + 1) * P)
-                for dh in range(DIM_HALVES):
-                    d_cols = slice(dh * BANK, (dh + 1) * BANK)
+        def quantise_gated(c, pair, g_grouped):
+            cols = slice(pair * 2 * P, (pair + 1) * 2 * P)
+            nc.vector.quantize_mx(
+                out=g_codes[:, c, cols].bitcast(FP8X4),
+                scales=g_scales[:, c, cols],
+                in_=g_grouped[:].rearrange("p i w -> p (i w)"),
+            )
+
+        def output_passes(c):
+            banks = []
+            for dh in range(DIM_HALVES):
+                bank = psum.tile([P, BANK], F32, tag="wide", bufs=6, name="o_bank")
+                d_cols = slice(dh * BANK, (dh + 1) * BANK)
+                for G in range(UV_PASSES):
+                    n_cols = slice(G * P, (G + 1) * P)
                     nc.tensor.matmul_mx(
-                        out=o_banks[cl * DIM_HALVES + dh][:],
-                        lhsT=g_codes[:, G, n_cols].bitcast(FP8X4),
-                        lhsT_scale=g_scales[:, G, n_cols],
+                        out=bank[:],
+                        lhsT=g_codes[:, c, n_cols].bitcast(FP8X4),
+                        lhsT_scale=g_scales[:, c, n_cols],
                         rhs=wo_codes[:, G, d_cols].bitcast(FP8X4),
                         rhs_scale=wo_scales[:, G, d_cols],
                         start=(G == 0),
                         stop=(G == UV_PASSES - 1),
                     )
+                banks.append(bank)
+            return banks
 
         def residual_and_bias(c, hid):
             o = stage.tile([P, DIM], F32, tag="o", bufs=4, name="o")
-            nc.vector.tensor_tensor(out=o[:], in0=hid[:, c % (TOKEN_TILES // 2), :], in1=bo_all[:], op=ALU.add)
+            nc.vector.tensor_tensor(out=o[:], in0=hid[:, c % 2, :], in1=bo_all[:], op=ALU.add)
             return o
 
-        def add_output(o, o_banks, cl):
+        def add_output(o, banks):
             for dh in range(DIM_HALVES):
                 d_cols = slice(dh * BANK, (dh + 1) * BANK)
-                nc.vector.tensor_tensor(out=o[:, d_cols], in0=o_banks[cl * DIM_HALVES + dh][:], in1=o[:, d_cols], op=ALU.add)
+                nc.vector.tensor_tensor(out=o[:, d_cols], in0=banks[dh][:], in1=o[:, d_cols], op=ALU.add)
 
-        def norm_and_store(c, o):
+        def sumsq(o):
             sum_sq = small.tile([P, 1], F32, tag="sum_sq", name="sum_sq")
             inv_rms = small.tile([P, 1], F32, tag="inv_rms", name="inv_rms")
             nc.scalar.activation(out=squares[:], in_=o[:], func=ACT.Square, accum_out=sum_sq[:])
             nc.scalar.activation(out=inv_rms[:], in_=sum_sq[:], func=ACT.Abs_reciprocal_sqrt, scale=1.0 / DIM, bias=eps[:])
+            return inv_rms
+        def scale_store(c, o, inv_rms):
             nc.scalar.activation(out=o[:], in_=o[:], func=ACT.Copy, scale=inv_rms[:])
             nc.sync.dma_start(out=out_view[c], in_=o[:])
 
         nc.sync.dma_start(out=k_sb[:], in_=k_view)
         nc.sync.dma_start(out=q_sb[:], in_=q_view)
         nc.gpsimd.dma_start(out=bo_all[:], in_=bo.partition_broadcast(P))
-        v_tiles = {0: load_v(0)}
-        u_tiles = {0: load_u(0)}
-        v_tiles[1] = load_v(1)
-        wo_tiles = {0: load_wo(0)}
-        u_tiles[1] = load_u(1)
-        wo_tiles[1] = load_wo(1)
-        hid_tiles = {}
+
+        v_tiles = {}
+        u_tiles = {}
+        for G in range(UV_PASSES):
+            for g in range(KEY_PASSES):
+                v_tiles[G, g] = load_v(G, g)
+            if G < 3:
+                u_tiles[G] = load_u(G)
+        wo_tiles = {G: load_wo(G) for G in range(2)}
 
         make_identity(nc, ident_bf[:])
         make_identity(nc, ident_f32[:])
@@ -249,81 +245,64 @@ def tile_gau_ae_pb_kernel(tc, q, k, u, v, hidden_states, Wo, bo, out):
         nc.scalar.activation(out=warm[:], in_=warm[:], func=ACT.Abs_reciprocal_sqrt)
 
         for g in range(KEY_PASSES):
-            bank = psum.tile([P, PACK, P], BF16, tag="bank", name="k_bank")
+            bank = psum.tile([P, PACK, P], BF16, tag="bank", bufs=2, name="k_bank")
             for t in range(PACK):
                 nc.tensor.transpose(bank[:, t, :], k_sb[:, g, t * KEY : (t + 1) * KEY], ident_bf[:])
-            nc.vector.tensor_copy(out=kT[:, g, :, :], in_=bank[:])
+            nc.scalar.copy(out=kT[:, g, :, :], in_=bank[:])
         for half in range(2):
-            tiles = TOKEN_TILES // 2
-            bank = psum.tile([P, tiles, P], BF16, tag="bank", name="q_bank")
+            tiles = TILES // 2
+            bank = psum.tile([P, tiles, P], BF16, tag="bank", bufs=2, name="q_bank")
             for cl in range(tiles):
                 nc.tensor.transpose(bank[:, cl, :], q_sb[:, half * tiles + cl, :], ident_bf[:])
             nc.scalar.copy(out=qT[:, half * tiles : (half + 1) * tiles, :], in_=bank[:])
 
-        at_tiles = {}
-        for g in range(KEY_PASSES):
-            at_tiles[g] = attention_weights(0, g)
-        quantise_v(0, v_tiles[0])
-        v_tiles[2] = load_v(2)
-        for g in range(KEY_PASSES):
-            quantise_attention_weights(0, g, at_tiles[g])
-        transpose_u(0, u_tiles[0])
-        u_tiles[2] = load_u(2)
+        uT = {}
 
-        steps = GROUPS * UV_PASSES
-        av_banks = values_passes(0)
+        def prepare_tile(c):
+            at_grouped = attention_weights(c)
+            uT[c] = transpose_u(c, u_tiles[c])
+            if c + 3 < TILES:
+                u_tiles[c + 3] = load_u(c + 3)
+            return at_grouped
+
+        def prepare_wo(G):
+            halves = [regroup_wo(nc.scalar.copy, wo_tiles[G], dh) for dh in range(DIM_HALVES)]
+            for dh in range(DIM_HALVES):
+                quantise_wo(G, dh, halves[dh])
+            if G + 2 < UV_PASSES:
+                wo_tiles[G + 2] = load_wo(G + 2)
+
+        for G in range(UV_PASSES):
+            v_grouped = [regroup_v(v_tiles[G, g]) for g in range(KEY_PASSES)]
+            at_grouped = prepare_tile(G)
+            for g in range(KEY_PASSES):
+                quantise_v(G, g, v_grouped[g])
+            quantise_attention_weights(G, at_grouped)
+            if G >= 2:
+                prepare_wo(G - 2)
+
+        hid_tiles = {part: load_hidden(part) for part in range(2)}
+
+        def finish_tile(c, o):
+            banks = output_passes(c)
+            add_output(o, banks)
+            scale_store(c, o, sumsq(o))
+
         o_tiles = {}
-        o_banks = {}
-        for step in range(steps):
-            tg, G = divmod(step, UV_PASSES)
-            if tg == 0:
-                if G == 0:
-                    for g in range(KEY_PASSES):
-                        at_tiles[g] = attention_weights(1, g)
-                by_scalar = regroup_wo(nc.scalar.copy, "by_scalar", wo_tiles[G], 1)
-                if G + 1 < GROUPS:
-                    transpose_u(G + 1, u_tiles[G + 1])
-                    if G + 3 < GROUPS:
-                        u_tiles[G + 3] = load_u(G + 3)
-                if G + 1 < UV_PASSES:
-                    quantise_v(G + 1, v_tiles[G + 1])
-                    if G + 3 < UV_PASSES:
-                        v_tiles[G + 3] = load_v(G + 3)
-                    else:
-                        hid_tiles[G + 3 - UV_PASSES] = load_hidden(G + 3 - UV_PASSES)
-                by_vector = regroup_wo(nc.vector.tensor_copy, "by_vector", wo_tiles[G], 0)
-                gate(step, av_banks)
-                quantise_wo(G, 0, by_vector)
-                if G == 0:
-                    for g in range(KEY_PASSES):
-                        quantise_attention_weights(1, g, at_tiles[g])
-                quantise_wo(G, 1, by_scalar)
-                if G + 2 < UV_PASSES:
-                    wo_tiles[G + 2] = load_wo(G + 2)
-            else:
-                if tg + 1 < GROUPS and G < KEY_PASSES:
-                    at_tiles[G] = attention_weights(tg + 1, G)
-                gate(step, av_banks)
-                if G == 0:
-                    for cl in range(GROUP_TILES):
-                        add_output(o_tiles[(tg - 1) * GROUP_TILES + cl], o_banks[tg - 1], cl)
-                if G < GROUP_TILES:
-                    c = (tg - 1) * GROUP_TILES + G
-                    norm_and_store(c, o_tiles[c])
-                if tg + 1 < GROUPS and G >= KEY_PASSES:
-                    quantise_attention_weights(tg + 1, G - KEY_PASSES, at_tiles[G - KEY_PASSES])
-            if G == 2:
-                for cl in range(GROUP_TILES):
-                    c = tg * GROUP_TILES + cl
-                    o_tiles[c] = residual_and_bias(c, hid_tiles[c // (TOKEN_TILES // 2)])
-            if step + 1 < steps:
-                av_banks = values_passes(step + 1)
-            if G == 0:
-                o_banks[tg] = [
-                    psum.tile([P, BANK], F32, tag="wide", name="o_bank%d" % i) for i in range(GROUP_TILES * DIM_HALVES)
-                ]
-            output_passes(step, o_banks[tg])
-        for cl in range(GROUP_TILES):
-            c = (GROUPS - 1) * GROUP_TILES + cl
-            add_output(o_tiles[c], o_banks[GROUPS - 1], cl)
-            norm_and_store(c, o_tiles[c])
+        for c in range(TILES):
+            banks = values_passes(c, 0)
+            g_first = gate(uT[c], 0, banks)
+            banks = values_passes(c, 1)
+            o_tiles[c] = residual_and_bias(c, hid_tiles[c // 2])
+            if c % 2 == 1 and c // 2 + 2 < TILES // 2:
+                hid_tiles[c // 2 + 2] = load_hidden(c // 2 + 2)
+            quantise_gated(c, 0, g_first)
+            g_second = gate(uT[c], 1, banks)
+            quantise_gated(c, 1, g_second)
+            if c < 2:
+                prepare_wo(c + 2)
+            if c + AHEAD < TILES:
+                quantise_attention_weights(c + AHEAD, prepare_tile(c + AHEAD))
+            if c > 0:
+                finish_tile(c - 1, o_tiles[c - 1])
+        finish_tile(TILES - 1, o_tiles[TILES - 1])

@@ -207,7 +207,9 @@ def tile_gau_ae_pb_kernel(tc, q, k, u, v, hidden_states, Wo, bo, out):
 
         def residual_and_bias(c, hid):
             o = stage.tile([P, DIM], F32, tag="o", bufs=4, name="o")
-            nc.vector.tensor_tensor(out=o[:], in0=hid[:, c % 2, :], in1=bo_all[:], op=ALU.add)
+            for dh in range(DIM_HALVES):
+                d_cols = slice(dh * BANK, (dh + 1) * BANK)
+                nc.gpsimd.tensor_tensor(out=o[:, d_cols], in0=hid[:, c % 2, d_cols], in1=bo_all[:, d_cols], op=ALU.add)
             return o
 
         def add_output(o, banks):
@@ -266,7 +268,7 @@ def tile_gau_ae_pb_kernel(tc, q, k, u, v, hidden_states, Wo, bo, out):
             return at_grouped
 
         def prepare_wo(G):
-            halves = [regroup_wo(nc.scalar.copy, wo_tiles[G], dh) for dh in range(DIM_HALVES)]
+            halves = [regroup_wo(nc.vector.tensor_copy, wo_tiles[G], 0), regroup_wo(nc.scalar.copy, wo_tiles[G], 1)]
             for dh in range(DIM_HALVES):
                 quantise_wo(G, dh, halves[dh])
             if G + 2 < UV_PASSES:

@@ -63,23 +63,25 @@ def tile_gau_ae_pb_kernel(tc, q, k, u, v, hidden_states, Wo, bo, out):
         v_scales = keep.tile([P, KEY_PASSES, UV], U8, align_bytes=64)
         wo_codes = keep.tile([P, UV_PASSES, DIM], U32, align_bytes=64)
         wo_scales = keep.tile([P, UV_PASSES, DIM], U8, align_bytes=64)
-        bo_all = keep.tile([P, DIM], BF16)
+        bo_all = keep.tile([P, DIM], F32)
+        bo_row = keep.tile([P, DIM], BF16)
+        ones = keep.tile([P, P], BF16)
         eps = keep.tile([P, 1], F32)
         warm = keep.tile([P, 1], F32)
         squares = keep.tile([P, DIM], BF16)
 
         def load_v(G, g):
-            v_raw = raw.tile([P, PACK, K_PASS], BF16, tag="v_raw", bufs=8, name="v_raw")
+            v_raw = raw.tile([P, PACK, K_PASS], BF16, tag="v_raw", bufs=7, name="v_raw")
             nc.sync.dma_start(out=v_raw[:], in_=v_view[g, :, :, G * K_PASS : (G + 1) * K_PASS])
             return v_raw
 
         def load_hidden(part):
-            hid = raw.tile([P, 2, DIM], BF16, tag="hid", bufs=2, name="hid")
+            hid = raw.tile([P, 2, DIM], BF16, tag="v_raw", bufs=7, name="hid")
             nc.sync.dma_start(out=hid[:], in_=hid_view[:, part * 2 : (part + 1) * 2, :])
             return hid
 
         def load_u(c):
-            u_raw = raw.tile([P, UV], BF16, tag="u_raw", bufs=3, name="u_raw")
+            u_raw = raw.tile([P, UV], BF16, tag="u_raw", bufs=4, name="u_raw")
             nc.sync.dma_start(out=u_raw[:], in_=u_view[:, c, :])
             return u_raw
 
@@ -106,17 +108,16 @@ def tile_gau_ae_pb_kernel(tc, q, k, u, v, hidden_states, Wo, bo, out):
         def quantise_attention_weights(c, at_grouped):
             nc.vector.quantize_mx(out=at_codes[:, c, :].bitcast(FP8X4), scales=at_scales[:, c, :], in_=at_grouped[:])
 
-        def regroup_v(v_raw):
-            v_grouped = stage.tile([P, PACK * K_PASS], BF16, tag="v_grouped", bufs=3, name="v_grouped", align_bytes=64)
+        def regroup_v(v_grouped, G, v_raw):
             for h in range(2):
+                first = (G % 2) * PACK * K_PASS + h * 1024
                 nc.vector.tensor_copy(
-                    out=v_grouped[:, h * 1024 : (h + 1) * 1024].rearrange("p (e w t) -> p e w t", e=2, t=PACK),
+                    out=v_grouped[:, first : first + 1024].rearrange("p (e w t) -> p e w t", e=2, t=PACK),
                     in_=v_raw[:, :, h * 256 : (h + 1) * 256].rearrange("p t (w e) -> p e w t", e=2),
                 )
-            return v_grouped
 
-        def quantise_v(G, g, v_grouped):
-            cols = slice(G * K_PASS, (G + 1) * K_PASS)
+        def quantise_v(pair, g, v_grouped):
+            cols = slice(pair * 2 * K_PASS, (pair + 1) * 2 * K_PASS)
             nc.vector.quantize_mx(out=v_codes[:, g, cols].bitcast(FP8X4), scales=v_scales[:, g, cols], in_=v_grouped[:])
 
         def regroup_wo(engine_copy, wo_raw, dh):
@@ -206,7 +207,7 @@ def tile_gau_ae_pb_kernel(tc, q, k, u, v, hidden_states, Wo, bo, out):
             return banks
 
         def residual_and_bias(c, hid):
-            o = stage.tile([P, DIM], F32, tag="o", bufs=4, name="o")
+            o = stage.tile([P, DIM], F32, tag="o", bufs=5, name="o")
             for dh in range(DIM_HALVES):
                 d_cols = slice(dh * BANK, (dh + 1) * BANK)
                 nc.gpsimd.tensor_tensor(out=o[:, d_cols], in0=hid[:, c % 2, d_cols], in1=bo_all[:, d_cols], op=ALU.add)
@@ -227,17 +228,18 @@ def tile_gau_ae_pb_kernel(tc, q, k, u, v, hidden_states, Wo, bo, out):
             nc.scalar.activation(out=o[:], in_=o[:], func=ACT.Copy, scale=inv_rms[:])
             nc.sync.dma_start(out=out_view[c], in_=o[:])
 
+        nc.gpsimd.memset(bo_row[:], 0.0)
+        nc.gpsimd.memset(ones[:], 1.0)
         nc.sync.dma_start(out=k_sb[:], in_=k_view)
         nc.sync.dma_start(out=q_sb[:], in_=q_view)
-        nc.gpsimd.dma_start(out=bo_all[:], in_=bo.partition_broadcast(P))
 
         v_tiles = {}
         u_tiles = {}
         for G in range(UV_PASSES):
             for g in range(KEY_PASSES):
                 v_tiles[G, g] = load_v(G, g)
-            if G < 3:
-                u_tiles[G] = load_u(G)
+            u_tiles[G] = load_u(G)
+        nc.sync.dma_start(out=bo_row[0:1, :], in_=bo.rearrange("(r d) -> r d", r=1))
         wo_tiles = {G: load_wo(G) for G in range(2)}
 
         make_identity(nc, ident_bf[:])
@@ -263,8 +265,8 @@ def tile_gau_ae_pb_kernel(tc, q, k, u, v, hidden_states, Wo, bo, out):
         def prepare_tile(c):
             at_grouped = attention_weights(c)
             uT[c] = transpose_u(c, u_tiles[c])
-            if c + 3 < TILES:
-                u_tiles[c + 3] = load_u(c + 3)
+            if c + UV_PASSES < TILES:
+                u_tiles[c + UV_PASSES] = load_u(c + UV_PASSES)
             return at_grouped
 
         def prepare_wo(G):
@@ -274,30 +276,68 @@ def tile_gau_ae_pb_kernel(tc, q, k, u, v, hidden_states, Wo, bo, out):
             if G + 2 < UV_PASSES:
                 wo_tiles[G + 2] = load_wo(G + 2)
 
-        for G in range(UV_PASSES):
-            v_grouped = [regroup_v(v_tiles[G, g]) for g in range(KEY_PASSES)]
-            at_grouped = prepare_tile(G)
-            for g in range(KEY_PASSES):
-                quantise_v(G, g, v_grouped[g])
-            quantise_attention_weights(G, at_grouped)
-            if G >= 2:
-                prepare_wo(G - 2)
+        with tc.manual_schedule(engines={mybir.EngineType.PE}):
+            for G in range(UV_PASSES):
+                if G % 2 == 0:
+                    v_grouped = [
+                        stage.tile([P, 2 * PACK * K_PASS], BF16, tag="v_grouped%d" % g, bufs=1, name="v_grouped", align_bytes=64)
+                        for g in range(KEY_PASSES)
+                    ]
+                for g in range(KEY_PASSES):
+                    regroup_v(v_grouped[g], G, v_tiles[G, g])
+                at_grouped = prepare_tile(G)
+                if G % 2 == 1:
+                    for g in range(KEY_PASSES):
+                        quantise_v(G // 2, g, v_grouped[g])
+                quantise_attention_weights(G, at_grouped)
+                if G >= 2:
+                    prepare_wo(G - 2)
+            first_banks = values_passes(0, 0)
 
         hid_tiles = {part: load_hidden(part) for part in range(2)}
+
+        for dh in range(DIM_HALVES):
+            d_cols = slice(dh * BANK, (dh + 1) * BANK)
+            bank = psum.tile([P, BANK], F32, tag="bank", bufs=2, name="bo_bank")
+            nc.tensor.matmul(out=bank[:], lhsT=ones[:], rhs=bo_row[:, d_cols], start=True, stop=True)
+            nc.scalar.copy(out=bo_all[:, d_cols], in_=bank[:])
 
         def finish_tile(c, o):
             banks = output_passes(c)
             add_output(o, banks)
             scale_store(c, o, sumsq(o))
 
+        def finish_tile_by_halves(c, o):
+            banks = output_passes(c)
+            sums = small.tile([P, DIM_HALVES], F32, tag="sums", name="sums")
+            for dh in range(DIM_HALVES):
+                d_cols = slice(dh * BANK, (dh + 1) * BANK)
+                nc.vector.tensor_tensor(out=o[:, d_cols], in0=banks[dh][:], in1=o[:, d_cols], op=ALU.add)
+                nc.scalar.activation(out=squares[:, d_cols], in_=o[:, d_cols], func=ACT.Square, accum_out=sums[:, dh : dh + 1])
+            sum_sq = small.tile([P, 1], F32, tag="sum_sq", name="sum_sq")
+            inv_rms = small.tile([P, 1], F32, tag="inv_rms", name="inv_rms")
+            nc.vector.tensor_tensor(out=sum_sq[:], in0=sums[:, 0:1], in1=sums[:, 1:2], op=ALU.add)
+            nc.scalar.activation(out=inv_rms[:], in_=sum_sq[:], func=ACT.Abs_reciprocal_sqrt, scale=1.0 / DIM, bias=eps[:])
+            nc.vector.tensor_scalar(out=o[:, BANK:], in0=o[:, BANK:], scalar1=inv_rms[:], scalar2=None, op0=ALU.mult)
+            nc.scalar.activation(out=o[:, :BANK], in_=o[:, :BANK], func=ACT.Copy, scale=inv_rms[:])
+            for dh in range(DIM_HALVES):
+                d_cols = slice(dh * BANK, (dh + 1) * BANK)
+                nc.sync.dma_start(out=out_view[c][:, d_cols], in_=o[:, d_cols])
+
         o_tiles = {}
-        for c in range(TILES):
-            banks = values_passes(c, 0)
-            g_first = gate(uT[c], 0, banks)
-            banks = values_passes(c, 1)
+
+        def next_residual(c):
             o_tiles[c] = residual_and_bias(c, hid_tiles[c // 2])
             if c % 2 == 1 and c // 2 + 2 < TILES // 2:
                 hid_tiles[c // 2 + 2] = load_hidden(c // 2 + 2)
+
+        next_residual(0)
+        for c in range(TILES):
+            banks = first_banks if c == 0 else values_passes(c, 0)
+            g_first = gate(uT[c], 0, banks)
+            banks = values_passes(c, 1)
+            if c + 1 < TILES:
+                next_residual(c + 1)
             quantise_gated(c, 0, g_first)
             g_second = gate(uT[c], 1, banks)
             quantise_gated(c, 1, g_second)
@@ -306,5 +346,5 @@ def tile_gau_ae_pb_kernel(tc, q, k, u, v, hidden_states, Wo, bo, out):
             if c + AHEAD < TILES:
                 quantise_attention_weights(c + AHEAD, prepare_tile(c + AHEAD))
             if c > 0:
-                finish_tile(c - 1, o_tiles[c - 1])
-        finish_tile(TILES - 1, o_tiles[TILES - 1])
+                (finish_tile if c < TILES - 1 else finish_tile_by_halves)(c - 1, o_tiles[c - 1])
+        finish_tile_by_halves(TILES - 1, o_tiles[TILES - 1])

@@ -57,8 +57,6 @@ def tile_gau_ae_pb_kernel(tc, q, k, u, v, hidden_states, Wo, bo, out):
         qT = keep.tile([P, TILES, P], BF16)
         at_codes = keep.tile([P, TILES, KEY_PASSES * P], U32, align_bytes=64)
         at_scales = keep.tile([P, TILES, KEY_PASSES * P], U8, align_bytes=64)
-        g_codes = keep.tile([P, TILES, UV_PASSES * P], U32, align_bytes=64)
-        g_scales = keep.tile([P, TILES, UV_PASSES * P], U8, align_bytes=64)
         v_codes = keep.tile([P, KEY_PASSES, UV], U32, align_bytes=64)
         v_scales = keep.tile([P, KEY_PASSES, UV], U8, align_bytes=64)
         wo_codes = keep.tile([P, UV_PASSES, DIM], U32, align_bytes=64)
@@ -90,7 +88,7 @@ def tile_gau_ae_pb_kernel(tc, q, k, u, v, hidden_states, Wo, bo, out):
             nc.sync.dma_start(out=wo_raw[:].rearrange("p (h e) d -> p h (e d)", h=2), in_=wo_view[G])
             return wo_raw
 
-        def attention_weights(c):
+        def attention_weights(c, at_grouped):
             relu = stage.tile([P, KEY_PASSES * BANK], F32, tag="relu", bufs=2, name="relu")
             for g in range(KEY_PASSES):
                 bank = psum.tile([P, PACK, P], F32, tag="bank", bufs=2, name="a_bank")
@@ -101,36 +99,38 @@ def tile_gau_ae_pb_kernel(tc, q, k, u, v, hidden_states, Wo, bo, out):
                     in_=bank[:].rearrange("p t n -> p n t"),
                     func=ACT.Relu,
                 )
-            at_grouped = stage.tile([P, KEY_PASSES * BANK], BF16, tag="at_grouped", bufs=3, name="at_grouped", align_bytes=64)
-            nc.scalar.activation(out=at_grouped[:], in_=relu[:], func=ACT.Square, scale=(KEY * TOKENS) ** -0.5)
-            return at_grouped
+            nc.scalar.activation(out=at_grouped[:, c % 2, :], in_=relu[:], func=ACT.Square, scale=(KEY * TOKENS) ** -0.5)
 
-        def quantise_attention_weights(c, at_grouped):
-            nc.vector.quantize_mx(out=at_codes[:, c, :].bitcast(FP8X4), scales=at_scales[:, c, :], in_=at_grouped[:])
+        def quantise_attention_weights(pair, at_grouped):
+            nc.vector.quantize_mx(
+                out=at_codes[:, 2 * pair : 2 * pair + 2, :].rearrange("p c w -> p (c w)").bitcast(FP8X4),
+                scales=at_scales[:, 2 * pair : 2 * pair + 2, :].rearrange("p c w -> p (c w)"),
+                in_=at_grouped[:].rearrange("p c w -> p (c w)"),
+            )
 
         def regroup_v(v_grouped, G, v_raw):
-            for h in range(2):
-                first = (G % 2) * PACK * K_PASS + h * 1024
-                nc.vector.tensor_copy(
-                    out=v_grouped[:, first : first + 1024].rearrange("p (e w t) -> p e w t", e=2, t=PACK),
-                    in_=v_raw[:, :, h * 256 : (h + 1) * 256].rearrange("p t (w e) -> p e w t", e=2),
-                )
+            first = (G % 2) * PACK * K_PASS
+            nc.vector.tensor_copy(
+                out=v_grouped[:, first : first + PACK * K_PASS].rearrange("p (e c i t) -> p c t i e", e=2, i=2, t=PACK),
+                in_=v_raw[:].rearrange("p t (c i e) -> p c t i e", i=2, e=2),
+            )
 
         def quantise_v(pair, g, v_grouped):
             cols = slice(pair * 2 * K_PASS, (pair + 1) * 2 * K_PASS)
             nc.vector.quantize_mx(out=v_codes[:, g, cols].bitcast(FP8X4), scales=v_scales[:, g, cols], in_=v_grouped[:])
 
-        def regroup_wo(engine_copy, wo_raw, dh):
-            wo_grouped = stage.tile([P, PACK * BANK], BF16, tag="wo_grouped", bufs=3, name="wo_grouped", align_bytes=64)
+        def regroup_wo(engine_copy, wo_grouped, wo_raw, dh):
             engine_copy(
-                out=wo_grouped[:].rearrange("p (c i t) -> p c t i", i=4, t=PACK),
+                out=wo_grouped[:, dh, :].rearrange("p (c i t) -> p c t i", i=4, t=PACK),
                 in_=wo_raw[:, :, dh * BANK : (dh + 1) * BANK].rearrange("p t (c i) -> p c t i", i=4),
             )
-            return wo_grouped
 
-        def quantise_wo(G, dh, wo_grouped):
-            cols = slice(dh * BANK, (dh + 1) * BANK)
-            nc.vector.quantize_mx(out=wo_codes[:, G, cols].bitcast(FP8X4), scales=wo_scales[:, G, cols], in_=wo_grouped[:])
+        def quantise_wo(G, wo_grouped):
+            nc.vector.quantize_mx(
+                out=wo_codes[:, G, :].bitcast(FP8X4),
+                scales=wo_scales[:, G, :],
+                in_=wo_grouped[:].rearrange("p h w -> p (h w)"),
+            )
 
         def transpose_u(c, u_raw):
             uT = stage.tile([P, UV_PASSES, P * 2], F32, tag="uT", bufs=5, name="uT")
@@ -153,7 +153,9 @@ def tile_gau_ae_pb_kernel(tc, q, k, u, v, hidden_states, Wo, bo, out):
                 G = 2 * pair + i
                 bank = psum.tile([P, PACK, P], F32, tag="wide", bufs=6, name="av_bank")
                 for j in range(PACK):
-                    e_cols = slice(G * K_PASS + j * P, G * K_PASS + (j + 1) * P)
+                    h, e = divmod(j, 2)
+                    first = G * K_PASS + (2 * e + h) * P
+                    e_cols = slice(first, first + P)
                     for g in range(KEY_PASSES):
                         n_cols = slice(g * P, (g + 1) * P)
                         nc.tensor.matmul_mx(
@@ -168,26 +170,25 @@ def tile_gau_ae_pb_kernel(tc, q, k, u, v, hidden_states, Wo, bo, out):
                 banks.append(bank)
             return banks
 
-        def gate(uT, pair, banks):
-            g_grouped = stage.tile([P, 2, BANK], BF16, tag="g_grouped", bufs=3, name="g_grouped", align_bytes=64)
+        def gate(uT, pair, banks, g_grouped):
             for i in range(2):
+                G = 2 * pair + i
                 nc.vector.tensor_tensor(
-                    out=g_grouped[:, i, :].rearrange("p (n j) -> p n j", j=PACK),
+                    out=g_grouped[:, G, :].rearrange("p (n j) -> p n j", j=PACK),
                     in0=banks[i][:].rearrange("p j n -> p n j"),
-                    in1=uT[:, 2 * pair + i, :].bitcast(BF16).rearrange("p (n j) -> p n j", j=PACK),
+                    in1=uT[:, G, :].bitcast(BF16).rearrange("p (n j) -> p n j", j=PACK),
                     op=ALU.mult,
                 )
-            return g_grouped
 
-        def quantise_gated(c, pair, g_grouped):
-            cols = slice(pair * 2 * P, (pair + 1) * 2 * P)
+        def quantise_gated(g_grouped, g_codes, g_scales, first, passes):
+            cols = slice(first * P, (first + passes) * P)
             nc.vector.quantize_mx(
-                out=g_codes[:, c, cols].bitcast(FP8X4),
-                scales=g_scales[:, c, cols],
-                in_=g_grouped[:].rearrange("p i w -> p (i w)"),
+                out=g_codes[:, cols].bitcast(FP8X4),
+                scales=g_scales[:, cols],
+                in_=g_grouped[:, first : first + passes, :].rearrange("p i w -> p (i w)"),
             )
 
-        def output_passes(c):
+        def output_passes(g_codes, g_scales):
             banks = []
             for dh in range(DIM_HALVES):
                 bank = psum.tile([P, BANK], F32, tag="wide", bufs=6, name="o_bank")
@@ -196,8 +197,8 @@ def tile_gau_ae_pb_kernel(tc, q, k, u, v, hidden_states, Wo, bo, out):
                     n_cols = slice(G * P, (G + 1) * P)
                     nc.tensor.matmul_mx(
                         out=bank[:],
-                        lhsT=g_codes[:, c, n_cols].bitcast(FP8X4),
-                        lhsT_scale=g_scales[:, c, n_cols],
+                        lhsT=g_codes[:, n_cols].bitcast(FP8X4),
+                        lhsT_scale=g_scales[:, n_cols],
                         rhs=wo_codes[:, G, d_cols].bitcast(FP8X4),
                         rhs_scale=wo_scales[:, G, d_cols],
                         start=(G == 0),
@@ -218,6 +219,13 @@ def tile_gau_ae_pb_kernel(tc, q, k, u, v, hidden_states, Wo, bo, out):
                 d_cols = slice(dh * BANK, (dh + 1) * BANK)
                 nc.vector.tensor_tensor(out=o[:, d_cols], in0=banks[dh][:], in1=o[:, d_cols], op=ALU.add)
 
+        def add_output_beside_vector(o, banks):
+            for dh in range(DIM_HALVES):
+                d_cols = slice(dh * BANK, (dh + 1) * BANK)
+                product = stage.tile([P, BANK], F32, tag="product", bufs=2, name="product")
+                nc.scalar.copy(out=product[:], in_=banks[dh][:])
+                nc.gpsimd.tensor_tensor(out=o[:, d_cols], in0=product[:], in1=o[:, d_cols], op=ALU.add)
+
         def sumsq(o):
             sum_sq = small.tile([P, 1], F32, tag="sum_sq", name="sum_sq")
             inv_rms = small.tile([P, 1], F32, tag="inv_rms", name="inv_rms")
@@ -231,14 +239,16 @@ def tile_gau_ae_pb_kernel(tc, q, k, u, v, hidden_states, Wo, bo, out):
         nc.gpsimd.memset(bo_row[:], 0.0)
         nc.gpsimd.memset(ones[:], 1.0)
         nc.sync.dma_start(out=k_sb[:], in_=k_view)
+        v_tiles = {(0, 0): load_v(0, 0)}
         nc.sync.dma_start(out=q_sb[:], in_=q_view)
-
-        v_tiles = {}
-        u_tiles = {}
-        for G in range(UV_PASSES):
+        for G, g in ((0, 1), (1, 0), (1, 1)):
+            v_tiles[G, g] = load_v(G, g)
+        u_tiles = {0: load_u(0)}
+        for G in range(2, UV_PASSES):
             for g in range(KEY_PASSES):
                 v_tiles[G, g] = load_v(G, g)
-            u_tiles[G] = load_u(G)
+            u_tiles[G - 1] = load_u(G - 1)
+        u_tiles[3] = load_u(3)
         nc.sync.dma_start(out=bo_row[0:1, :], in_=bo.rearrange("(r d) -> r d", r=1))
         wo_tiles = {G: load_wo(G) for G in range(2)}
 
@@ -261,18 +271,23 @@ def tile_gau_ae_pb_kernel(tc, q, k, u, v, hidden_states, Wo, bo, out):
             nc.scalar.copy(out=qT[:, half * tiles : (half + 1) * tiles, :], in_=bank[:])
 
         uT = {}
+        at_pair = {}
 
         def prepare_tile(c):
-            at_grouped = attention_weights(c)
+            if c % 2 == 0:
+                at_pair[0] = stage.tile([P, 2, KEY_PASSES * BANK], BF16, tag="at_grouped", bufs=2, name="at_grouped", align_bytes=64)
+            attention_weights(c, at_pair[0])
             uT[c] = transpose_u(c, u_tiles[c])
             if c + UV_PASSES < TILES:
                 u_tiles[c + UV_PASSES] = load_u(c + UV_PASSES)
-            return at_grouped
+            if c % 2 == 1:
+                quantise_attention_weights(c // 2, at_pair[0])
 
         def prepare_wo(G):
-            halves = [regroup_wo(nc.vector.tensor_copy, wo_tiles[G], 0), regroup_wo(nc.scalar.copy, wo_tiles[G], 1)]
-            for dh in range(DIM_HALVES):
-                quantise_wo(G, dh, halves[dh])
+            wo_grouped = stage.tile([P, DIM_HALVES, PACK * BANK], BF16, tag="wo_grouped", bufs=2, name="wo_grouped", align_bytes=64)
+            regroup_wo(nc.vector.tensor_copy, wo_grouped, wo_tiles[G], 0)
+            regroup_wo(nc.scalar.copy, wo_grouped, wo_tiles[G], 1)
+            quantise_wo(G, wo_grouped)
             if G + 2 < UV_PASSES:
                 wo_tiles[G + 2] = load_wo(G + 2)
 
@@ -285,11 +300,10 @@ def tile_gau_ae_pb_kernel(tc, q, k, u, v, hidden_states, Wo, bo, out):
                     ]
                 for g in range(KEY_PASSES):
                     regroup_v(v_grouped[g], G, v_tiles[G, g])
-                at_grouped = prepare_tile(G)
+                prepare_tile(G)
                 if G % 2 == 1:
                     for g in range(KEY_PASSES):
                         quantise_v(G // 2, g, v_grouped[g])
-                quantise_attention_weights(G, at_grouped)
                 if G >= 2:
                     prepare_wo(G - 2)
             first_banks = values_passes(0, 0)
@@ -303,12 +317,14 @@ def tile_gau_ae_pb_kernel(tc, q, k, u, v, hidden_states, Wo, bo, out):
             nc.scalar.copy(out=bo_all[:, d_cols], in_=bank[:])
 
         def finish_tile(c, o):
-            banks = output_passes(c)
-            add_output(o, banks)
+            banks = output_passes(*g_mx[c])
+            if 3 <= c < 5:
+                add_output_beside_vector(o, banks)
+            else:
+                add_output(o, banks)
             scale_store(c, o, sumsq(o))
 
-        def finish_tile_by_halves(c, o):
-            banks = output_passes(c)
+        def finish_tile_by_halves(c, o, banks):
             sums = small.tile([P, DIM_HALVES], F32, tag="sums", name="sums")
             for dh in range(DIM_HALVES):
                 d_cols = slice(dh * BANK, (dh + 1) * BANK)
@@ -318,13 +334,17 @@ def tile_gau_ae_pb_kernel(tc, q, k, u, v, hidden_states, Wo, bo, out):
             inv_rms = small.tile([P, 1], F32, tag="inv_rms", name="inv_rms")
             nc.vector.tensor_tensor(out=sum_sq[:], in0=sums[:, 0:1], in1=sums[:, 1:2], op=ALU.add)
             nc.scalar.activation(out=inv_rms[:], in_=sum_sq[:], func=ACT.Abs_reciprocal_sqrt, scale=1.0 / DIM, bias=eps[:])
-            nc.vector.tensor_scalar(out=o[:, BANK:], in0=o[:, BANK:], scalar1=inv_rms[:], scalar2=None, op0=ALU.mult)
-            nc.scalar.activation(out=o[:, :BANK], in_=o[:, :BANK], func=ACT.Copy, scale=inv_rms[:])
+            if c < TILES - 1:
+                nc.vector.tensor_scalar(out=o[:], in0=o[:], scalar1=inv_rms[:], scalar2=None, op0=ALU.mult)
+            else:
+                nc.vector.tensor_scalar(out=o[:, BANK:], in0=o[:, BANK:], scalar1=inv_rms[:], scalar2=None, op0=ALU.mult)
+                nc.scalar.activation(out=o[:, :BANK], in_=o[:, :BANK], func=ACT.Copy, scale=inv_rms[:])
             for dh in range(DIM_HALVES):
                 d_cols = slice(dh * BANK, (dh + 1) * BANK)
                 nc.sync.dma_start(out=out_view[c][:, d_cols], in_=o[:, d_cols])
 
         o_tiles = {}
+        g_mx = {}
 
         def next_residual(c):
             o_tiles[c] = residual_and_bias(c, hid_tiles[c // 2])
@@ -334,17 +354,25 @@ def tile_gau_ae_pb_kernel(tc, q, k, u, v, hidden_states, Wo, bo, out):
         next_residual(0)
         for c in range(TILES):
             banks = first_banks if c == 0 else values_passes(c, 0)
-            g_first = gate(uT[c], 0, banks)
+            g_grouped = stage.tile([P, UV_PASSES, BANK], BF16, tag="g_grouped", bufs=3, name="g_grouped", align_bytes=64)
+            gate(uT[c], 0, banks, g_grouped)
             banks = values_passes(c, 1)
             if c + 1 < TILES:
                 next_residual(c + 1)
-            quantise_gated(c, 0, g_first)
-            g_second = gate(uT[c], 1, banks)
-            quantise_gated(c, 1, g_second)
+            g_codes = stage.tile([P, UV_PASSES * P], U32, tag="g_codes", bufs=3, name="g_codes", align_bytes=64)
+            g_scales = stage.tile([P, UV_PASSES * P], U8, tag="g_scales", bufs=3, name="g_scales", align_bytes=64)
+            parts = PAIRS if c == TILES - 1 else 1
+            if parts == PAIRS:
+                quantise_gated(g_grouped, g_codes, g_scales, 0, 2)
+            gate(uT[c], 1, banks, g_grouped)
+            first = UV_PASSES - UV_PASSES // parts
+            quantise_gated(g_grouped, g_codes, g_scales, first, UV_PASSES - first)
+            g_mx[c] = (g_codes, g_scales)
             if c < 2:
                 prepare_wo(c + 2)
             if c + AHEAD < TILES:
-                quantise_attention_weights(c + AHEAD, prepare_tile(c + AHEAD))
-            if c > 0:
-                (finish_tile if c < TILES - 1 else finish_tile_by_halves)(c - 1, o_tiles[c - 1])
-        finish_tile_by_halves(TILES - 1, o_tiles[TILES - 1])
+                prepare_tile(c + AHEAD)
+            if 0 < c < TILES - 1:
+                finish_tile(c - 1, o_tiles[c - 1])
+        for c in range(TILES - 2, TILES):
+            finish_tile_by_halves(c, o_tiles[c], output_passes(*g_mx[c]))

@@ -25,6 +25,7 @@ NORM_EPS = 1e-12
 TILES = TOKENS // P
 KEY_PASSES = TOKENS // K_PASS
 UV_PASSES = UV // K_PASS
+V_BUFS = {K_PASS: 4, 2 * K_PASS: 2}
 PAIRS = UV_PASSES // 2
 DIM_HALVES = DIM // BANK
 AHEAD = UV_PASSES
@@ -43,10 +44,10 @@ def tile_gau_ae_pb_kernel(tc, q, k, u, v, hidden_states, Wo, bo, out):
 
         k_view = k.flatten_outer_dims().rearrange("(g p t) d -> p g (t d)", g=KEY_PASSES, p=P, t=PACK)
         v_view = v.flatten_outer_dims().rearrange("(g p t) e -> g p t e", g=KEY_PASSES, p=P, t=PACK)
-        q_view = q.flatten_outer_dims().rearrange("(c p) d -> p c d", p=P)
-        u_view = u.flatten_outer_dims().rearrange("(c p) e -> p c e", p=P)
-        hid_view = hidden_states.flatten_outer_dims().rearrange("(c p) d -> p c d", p=P)
-        out_view = out.flatten_outer_dims().rearrange("(c p) d -> c p d", p=P)
+        q_view = q.flatten_outer_dims().rearrange("(p c) d -> p c d", p=P)
+        u_view = u.flatten_outer_dims().rearrange("(p c) e -> p c e", p=P)
+        hid_view = hidden_states.flatten_outer_dims().rearrange("(p c) d -> p c d", p=P)
+        out_view = out.flatten_outer_dims().rearrange("(p c) d -> c p d", p=P)
         wo_view = Wo.rearrange("(G h p e) d -> G p h (e d)", G=UV_PASSES, h=2, p=P, e=2)
 
         ident_bf = keep.tile([P, P], BF16)
@@ -68,14 +69,15 @@ def tile_gau_ae_pb_kernel(tc, q, k, u, v, hidden_states, Wo, bo, out):
         warm = keep.tile([P, 1], F32)
         squares = keep.tile([P, DIM], BF16)
 
-        def load_v(G, g):
-            v_raw = raw.tile([P, PACK, K_PASS], BF16, tag="v_raw", bufs=7, name="v_raw")
-            nc.sync.dma_start(out=v_raw[:], in_=v_view[g, :, :, G * K_PASS : (G + 1) * K_PASS])
+        def load_v(first, width, g):
+            tag = "v_raw%d" % width
+            v_raw = raw.tile([P, PACK, width], BF16, tag=tag, bufs=V_BUFS[width], name="v_raw")
+            nc.sync.dma_start(out=v_raw[:], in_=v_view[g, :, :, first : first + width])
             return v_raw
 
         def load_hidden(part):
-            hid = raw.tile([P, 2, DIM], BF16, tag="v_raw", bufs=7, name="hid")
-            nc.sync.dma_start(out=hid[:], in_=hid_view[:, part * 2 : (part + 1) * 2, :])
+            hid = raw.tile([P, TILES // 2, DIM], BF16, tag="v_raw%d" % (2 * K_PASS), bufs=V_BUFS[2 * K_PASS], name="hid")
+            nc.sync.dma_start(out=hid[:], in_=hid_view[:, part * (TILES // 2) : (part + 1) * (TILES // 2), :])
             return hid
 
         def load_u(c):
@@ -108,12 +110,16 @@ def tile_gau_ae_pb_kernel(tc, q, k, u, v, hidden_states, Wo, bo, out):
                 in_=at_grouped[:].rearrange("p c w -> p (c w)"),
             )
 
-        def regroup_v(v_grouped, G, v_raw):
-            first = (G % 2) * PACK * K_PASS
-            nc.vector.tensor_copy(
-                out=v_grouped[:, first : first + PACK * K_PASS].rearrange("p (e c i t) -> p c t i e", e=2, i=2, t=PACK),
-                in_=v_raw[:].rearrange("p t (c i e) -> p c t i e", i=2, e=2),
-            )
+        def regroup_v(v_raws):
+            v_grouped = stage.tile([P, 2 * PACK * K_PASS], BF16, tag="v_grouped", bufs=2, name="v_grouped", align_bytes=64)
+            grouped = v_grouped[:].rearrange("p (e c i t) -> p c t i e", e=2, i=2, t=PACK)
+            step = K_PASS // 2 // len(v_raws)
+            for i, v_raw in enumerate(v_raws):
+                nc.vector.tensor_copy(
+                    out=grouped[:, i * step : (i + 1) * step, :, :, :],
+                    in_=v_raw[:].rearrange("p t (c i e) -> p c t i e", i=2, e=2),
+                )
+            return v_grouped
 
         def quantise_v(pair, g, v_grouped):
             cols = slice(pair * 2 * K_PASS, (pair + 1) * 2 * K_PASS)
@@ -133,7 +139,7 @@ def tile_gau_ae_pb_kernel(tc, q, k, u, v, hidden_states, Wo, bo, out):
             )
 
         def transpose_u(c, u_raw):
-            uT = stage.tile([P, UV_PASSES, P * 2], F32, tag="uT", bufs=5, name="uT")
+            uT = stage.tile([P, UV_PASSES, P * 2], F32, tag="uT", bufs=4, name="uT")
             words = u_raw[:].bitcast(F32)
             for pair in range(PAIRS):
                 bank = psum.tile([P, 2, 2, P], F32, tag="bank", bufs=2, name="u_bank")
@@ -154,7 +160,7 @@ def tile_gau_ae_pb_kernel(tc, q, k, u, v, hidden_states, Wo, bo, out):
                 bank = psum.tile([P, PACK, P], F32, tag="wide", bufs=6, name="av_bank")
                 for j in range(PACK):
                     h, e = divmod(j, 2)
-                    first = G * K_PASS + (2 * e + h) * P
+                    first = (G // 2) * 2 * K_PASS + e * K_PASS + (G % 2) * 2 * P + h * P
                     e_cols = slice(first, first + P)
                     for g in range(KEY_PASSES):
                         n_cols = slice(g * P, (g + 1) * P)
@@ -211,20 +217,13 @@ def tile_gau_ae_pb_kernel(tc, q, k, u, v, hidden_states, Wo, bo, out):
             o = stage.tile([P, DIM], F32, tag="o", bufs=5, name="o")
             for dh in range(DIM_HALVES):
                 d_cols = slice(dh * BANK, (dh + 1) * BANK)
-                nc.gpsimd.tensor_tensor(out=o[:, d_cols], in0=hid[:, c % 2, d_cols], in1=bo_all[:, d_cols], op=ALU.add)
+                nc.gpsimd.tensor_tensor(out=o[:, d_cols], in0=hid[:, c % (TILES // 2), d_cols], in1=bo_all[:, d_cols], op=ALU.add)
             return o
 
         def add_output(o, banks):
             for dh in range(DIM_HALVES):
                 d_cols = slice(dh * BANK, (dh + 1) * BANK)
                 nc.vector.tensor_tensor(out=o[:, d_cols], in0=banks[dh][:], in1=o[:, d_cols], op=ALU.add)
-
-        def add_output_beside_vector(o, banks):
-            for dh in range(DIM_HALVES):
-                d_cols = slice(dh * BANK, (dh + 1) * BANK)
-                product = stage.tile([P, BANK], F32, tag="product", bufs=2, name="product")
-                nc.scalar.copy(out=product[:], in_=banks[dh][:])
-                nc.gpsimd.tensor_tensor(out=o[:, d_cols], in0=product[:], in1=o[:, d_cols], op=ALU.add)
 
         def sumsq(o):
             sum_sq = small.tile([P, 1], F32, tag="sum_sq", name="sum_sq")
@@ -239,15 +238,14 @@ def tile_gau_ae_pb_kernel(tc, q, k, u, v, hidden_states, Wo, bo, out):
         nc.gpsimd.memset(bo_row[:], 0.0)
         nc.gpsimd.memset(ones[:], 1.0)
         nc.sync.dma_start(out=k_sb[:], in_=k_view)
-        v_tiles = {(0, 0): load_v(0, 0)}
+        v_tiles = {(0, 0): [load_v(0, K_PASS, 0)]}
         nc.sync.dma_start(out=q_sb[:], in_=q_view)
-        for G, g in ((0, 1), (1, 0), (1, 1)):
-            v_tiles[G, g] = load_v(G, g)
+        v_tiles[0, 0].append(load_v(K_PASS, K_PASS, 0))
+        v_tiles[0, 1] = [load_v(i * K_PASS, K_PASS, 1) for i in range(2)]
         u_tiles = {0: load_u(0)}
-        for G in range(2, UV_PASSES):
-            for g in range(KEY_PASSES):
-                v_tiles[G, g] = load_v(G, g)
-            u_tiles[G - 1] = load_u(G - 1)
+        for g in range(KEY_PASSES):
+            v_tiles[1, g] = [load_v(2 * K_PASS, 2 * K_PASS, g)]
+            u_tiles[g + 1] = load_u(g + 1)
         u_tiles[3] = load_u(3)
         nc.sync.dma_start(out=bo_row[0:1, :], in_=bo.rearrange("(r d) -> r d", r=1))
         wo_tiles = {G: load_wo(G) for G in range(2)}
@@ -292,18 +290,12 @@ def tile_gau_ae_pb_kernel(tc, q, k, u, v, hidden_states, Wo, bo, out):
                 wo_tiles[G + 2] = load_wo(G + 2)
 
         with tc.manual_schedule(engines={mybir.EngineType.PE}):
+            v_parts = []
             for G in range(UV_PASSES):
-                if G % 2 == 0:
-                    v_grouped = [
-                        stage.tile([P, 2 * PACK * K_PASS], BF16, tag="v_grouped%d" % g, bufs=1, name="v_grouped", align_bytes=64)
-                        for g in range(KEY_PASSES)
-                    ]
-                for g in range(KEY_PASSES):
-                    regroup_v(v_grouped[g], G, v_tiles[G, g])
+                v_parts.append(regroup_v(v_tiles[divmod(G, KEY_PASSES)]))
                 prepare_tile(G)
-                if G % 2 == 1:
-                    for g in range(KEY_PASSES):
-                        quantise_v(G // 2, g, v_grouped[g])
+                for i in range(max(G - 1, 0), G if G < UV_PASSES - 1 else UV_PASSES):
+                    quantise_v(*divmod(i, KEY_PASSES), v_parts[i])
                 if G >= 2:
                     prepare_wo(G - 2)
             first_banks = values_passes(0, 0)
@@ -318,10 +310,7 @@ def tile_gau_ae_pb_kernel(tc, q, k, u, v, hidden_states, Wo, bo, out):
 
         def finish_tile(c, o):
             banks = output_passes(*g_mx[c])
-            if 3 <= c < 5:
-                add_output_beside_vector(o, banks)
-            else:
-                add_output(o, banks)
+            add_output(o, banks)
             scale_store(c, o, sumsq(o))
 
         def finish_tile_by_halves(c, o, banks):
@@ -347,14 +336,12 @@ def tile_gau_ae_pb_kernel(tc, q, k, u, v, hidden_states, Wo, bo, out):
         g_mx = {}
 
         def next_residual(c):
-            o_tiles[c] = residual_and_bias(c, hid_tiles[c // 2])
-            if c % 2 == 1 and c // 2 + 2 < TILES // 2:
-                hid_tiles[c // 2 + 2] = load_hidden(c // 2 + 2)
+            o_tiles[c] = residual_and_bias(c, hid_tiles[c // (TILES // 2)])
 
         next_residual(0)
         for c in range(TILES):
             banks = first_banks if c == 0 else values_passes(c, 0)
-            g_grouped = stage.tile([P, UV_PASSES, BANK], BF16, tag="g_grouped", bufs=3, name="g_grouped", align_bytes=64)
+            g_grouped = stage.tile([P, UV_PASSES, BANK], BF16, tag="g_grouped", bufs=2, name="g_grouped", align_bytes=64)
             gate(uT[c], 0, banks, g_grouped)
             banks = values_passes(c, 1)
             if c + 1 < TILES:

@@ -139,7 +139,7 @@ def tile_gau_ae_pb_kernel(tc, q, k, u, v, hidden_states, Wo, bo, out):
             )
 
         def transpose_u(c, u_raw):
-            uT = stage.tile([P, UV_PASSES, P * 2], F32, tag="uT", bufs=4, name="uT")
+            uT = stage.tile([P, UV_PASSES, P * 2], F32, tag="uT", bufs=5, name="uT")
             words = u_raw[:].bitcast(F32)
             for pair in range(PAIRS):
                 bank = psum.tile([P, 2, 2, P], F32, tag="bank", bufs=2, name="u_bank")
@@ -214,7 +214,7 @@ def tile_gau_ae_pb_kernel(tc, q, k, u, v, hidden_states, Wo, bo, out):
             return banks
 
         def residual_and_bias(c, hid):
-            o = stage.tile([P, DIM], F32, tag="o", bufs=5, name="o")
+            o = stage.tile([P, DIM], F32, tag="o", bufs=4, name="o")
             for dh in range(DIM_HALVES):
                 d_cols = slice(dh * BANK, (dh + 1) * BANK)
                 nc.gpsimd.tensor_tensor(out=o[:, d_cols], in0=hid[:, c % (TILES // 2), d_cols], in1=bo_all[:, d_cols], op=ALU.add)
@@ -341,7 +341,7 @@ def tile_gau_ae_pb_kernel(tc, q, k, u, v, hidden_states, Wo, bo, out):
         next_residual(0)
         for c in range(TILES):
             banks = first_banks if c == 0 else values_passes(c, 0)
-            g_grouped = stage.tile([P, UV_PASSES, BANK], BF16, tag="g_grouped", bufs=2, name="g_grouped", align_bytes=64)
+            g_grouped = stage.tile([P, UV_PASSES, BANK], BF16, tag="g_grouped", bufs=3, name="g_grouped", align_bytes=64)
             gate(uT[c], 0, banks, g_grouped)
             banks = values_passes(c, 1)
             if c + 1 < TILES:

@@ -319,18 +319,20 @@ def tile_gau_ae_pb_kernel(tc, q, k, u, v, hidden_states, Wo, bo, out):
                 d_cols = slice(dh * BANK, (dh + 1) * BANK)
                 nc.vector.tensor_tensor(out=o[:, d_cols], in0=banks[dh][:], in1=o[:, d_cols], op=ALU.add)
                 nc.scalar.activation(out=squares[:, d_cols], in_=o[:, d_cols], func=ACT.Square, accum_out=sums[:, dh : dh + 1])
-            sum_sq = small.tile([P, 1], F32, tag="sum_sq", name="sum_sq")
+            first_mean = small.tile([P, 1], F32, tag="first_mean", name="first_mean")
             inv_rms = small.tile([P, 1], F32, tag="inv_rms", name="inv_rms")
-            nc.vector.tensor_tensor(out=sum_sq[:], in0=sums[:, 0:1], in1=sums[:, 1:2], op=ALU.add)
-            nc.scalar.activation(out=inv_rms[:], in_=sum_sq[:], func=ACT.Abs_reciprocal_sqrt, scale=1.0 / DIM, bias=eps[:])
-            if c < TILES - 1:
-                nc.vector.tensor_scalar(out=o[:], in0=o[:], scalar1=inv_rms[:], scalar2=None, op0=ALU.mult)
-            else:
-                nc.vector.tensor_scalar(out=o[:, BANK:], in0=o[:, BANK:], scalar1=inv_rms[:], scalar2=None, op0=ALU.mult)
-                nc.scalar.activation(out=o[:, :BANK], in_=o[:, :BANK], func=ACT.Copy, scale=inv_rms[:])
-            for dh in range(DIM_HALVES):
-                d_cols = slice(dh * BANK, (dh + 1) * BANK)
-                nc.sync.dma_start(out=out_view[c][:, d_cols], in_=o[:, d_cols])
+            nc.vector.tensor_scalar(
+                out=first_mean[:], in0=sums[:, 0:1], scalar1=1.0 / DIM, scalar2=NORM_EPS, op0=ALU.mult, op1=ALU.add
+            )
+            nc.scalar.activation(
+                out=inv_rms[:], in_=sums[:, 1:2], func=ACT.Abs_reciprocal_sqrt, scale=1.0 / DIM, bias=first_mean[:]
+            )
+            split = 3 * DIM // 8 if c == TILES - 1 else 0
+            nc.vector.tensor_scalar(out=o[:, split:], in0=o[:, split:], scalar1=inv_rms[:], scalar2=None, op0=ALU.mult)
+            nc.sync.dma_start(out=out_view[c][:, split:], in_=o[:, split:])
+            if split > 0:
+                nc.scalar.activation(out=o[:, :split], in_=o[:, :split], func=ACT.Copy, scale=inv_rms[:])
+                nc.sync.dma_start(out=out_view[c][:, :split], in_=o[:, :split])
 
         o_tiles = {}
         g_mx = {}

from contextlib import ExitStack

import concourse.mybir as mybir
from concourse.masks import make_identity

F32 = mybir.dt.float32
BF16 = mybir.dt.bfloat16
U32 = mybir.dt.uint32
U8 = mybir.dt.uint8
FP8X4 = mybir.dt.float8_e4m3fn_x4
ACT = mybir.ActivationFunctionType
ALU = mybir.AluOpType

P = 128
PACK = 4
K_PASS = P * PACK
BANK = 512

TOKENS = 1024
KEY = 128
UV = 2048
DIM = 1024
NORM_EPS = 1e-12

TILES = TOKENS // P
KEY_PASSES = TOKENS // K_PASS
UV_PASSES = UV // K_PASS
V_BUFS = {K_PASS: 4, 2 * K_PASS: 2}
PAIRS = UV_PASSES // 2
DIM_HALVES = DIM // BANK
AHEAD = UV_PASSES

FLOPS = 2 * TOKENS * TOKENS * KEY + 2 * 2 * TOKENS * TOKENS * UV


def tile_gau_ae_pb_kernel(tc, q, k, u, v, hidden_states, Wo, bo, out):
    nc = tc.nc
    with ExitStack() as ctx:
        keep = ctx.enter_context(tc.tile_pool(name="keep", bufs=1))
        raw = ctx.enter_context(tc.tile_pool(name="raw", bufs=2))
        stage = ctx.enter_context(tc.tile_pool(name="stage", bufs=2))
        small = ctx.enter_context(tc.tile_pool(name="small", bufs=3))
        psum = ctx.enter_context(tc.psum_pool(name="psum", bufs=2))

        k_view = k.flatten_outer_dims().rearrange("(g p t) d -> p g (t d)", g=KEY_PASSES, p=P, t=PACK)
        v_view = v.flatten_outer_dims().rearrange("(g p t) e -> g p t e", g=KEY_PASSES, p=P, t=PACK)
        q_view = q.flatten_outer_dims().rearrange("(p c) d -> p c d", p=P)
        u_view = u.flatten_outer_dims().rearrange("(p c) e -> p c e", p=P)
        hid_view = hidden_states.flatten_outer_dims().rearrange("(p c) d -> p c d", p=P)
        out_view = out.flatten_outer_dims().rearrange("(p c) d -> c p d", p=P)
        wo_view = Wo.rearrange("(G h p e) d -> G p h (e d)", G=UV_PASSES, h=2, p=P, e=2)

        ident_bf = keep.tile([P, P], BF16)
        ident_f32 = keep.tile([P, P], F32)
        k_sb = keep.tile([P, KEY_PASSES, PACK * KEY], BF16)
        q_sb = keep.tile([P, TILES, KEY], BF16)
        kT = keep.tile([P, KEY_PASSES, PACK, P], BF16)
        qT = keep.tile([P, TILES, P], BF16)
        at_codes = keep.tile([P, TILES, KEY_PASSES * P], U32, align_bytes=64)
        at_scales = keep.tile([P, TILES, KEY_PASSES * P], U8, align_bytes=64)
        v_codes = keep.tile([P, KEY_PASSES, UV], U32, align_bytes=64)
        v_scales = keep.tile([P, KEY_PASSES, UV], U8, align_bytes=64)
        wo_codes = keep.tile([P, UV_PASSES, DIM], U32, align_bytes=64)
        wo_scales = keep.tile([P, UV_PASSES, DIM], U8, align_bytes=64)
        bo_all = keep.tile([P, DIM], F32)
        bo_row = keep.tile([P, DIM], BF16)
        ones = keep.tile([P, P], BF16)
        eps = keep.tile([P, 1], F32)
        warm = keep.tile([P, 1], F32)
        squares = keep.tile([P, DIM], BF16)

        def load_v(first, width, g):
            tag = "v_raw%d" % width
            v_raw = raw.tile([P, PACK, width], BF16, tag=tag, bufs=V_BUFS[width], name="v_raw")
            nc.sync.dma_start(out=v_raw[:], in_=v_view[g, :, :, first : first + width])
            return v_raw

        def load_hidden(part):
            hid = raw.tile([P, TILES // 2, DIM], BF16, tag="v_raw%d" % (2 * K_PASS), bufs=V_BUFS[2 * K_PASS], name="hid")
            nc.sync.dma_start(out=hid[:], in_=hid_view[:, part * (TILES // 2) : (part + 1) * (TILES // 2), :])
            return hid

        def load_u(c):
            u_raw = raw.tile([P, UV], BF16, tag="u_raw", bufs=4, name="u_raw")
            nc.sync.dma_start(out=u_raw[:], in_=u_view[:, c, :])
            return u_raw

        def load_wo(G):
            wo_raw = raw.tile([P, PACK, DIM], BF16, tag="wo_raw", bufs=2, name="wo_raw")
            nc.sync.dma_start(out=wo_raw[:].rearrange("p (h e) d -> p h (e d)", h=2), in_=wo_view[G])
            return wo_raw

        def attention_weights(c, at_grouped):
            relu = stage.tile([P, KEY_PASSES * BANK], F32, tag="relu", bufs=2, name="relu")
            for g in range(KEY_PASSES):
                bank = psum.tile([P, PACK, P], F32, tag="bank", bufs=2, name="a_bank")
                for t in range(PACK):
                    nc.tensor.matmul(out=bank[:, t, :], lhsT=kT[:, g, t, :], rhs=qT[:, c, :], start=True, stop=True)
                nc.scalar.activation(
                    out=relu[:, g * BANK : (g + 1) * BANK].rearrange("p (n t) -> p n t", t=PACK),
                    in_=bank[:].rearrange("p t n -> p n t"),
                    func=ACT.Relu,
                )
            nc.scalar.activation(out=at_grouped[:, c % 2, :], in_=relu[:], func=ACT.Square, scale=(KEY * TOKENS) ** -0.5)

        def quantise_attention_weights(pair, at_grouped):
            nc.vector.quantize_mx(
                out=at_codes[:, 2 * pair : 2 * pair + 2, :].rearrange("p c w -> p (c w)").bitcast(FP8X4),
                scales=at_scales[:, 2 * pair : 2 * pair + 2, :].rearrange("p c w -> p (c w)"),
                in_=at_grouped[:].rearrange("p c w -> p (c w)"),
            )

        def regroup_v(v_raws):
            v_grouped = stage.tile([P, 2 * PACK * K_PASS], BF16, tag="v_grouped", bufs=2, name="v_grouped", align_bytes=64)
            grouped = v_grouped[:].rearrange("p (e c i t) -> p c t i e", e=2, i=2, t=PACK)
            step = K_PASS // 2 // len(v_raws)
            for i, v_raw in enumerate(v_raws):
                nc.vector.tensor_copy(
                    out=grouped[:, i * step : (i + 1) * step, :, :, :],
                    in_=v_raw[:].rearrange("p t (c i e) -> p c t i e", i=2, e=2),
                )
            return v_grouped

        def quantise_v(pair, g, v_grouped):
            cols = slice(pair * 2 * K_PASS, (pair + 1) * 2 * K_PASS)
            nc.vector.quantize_mx(out=v_codes[:, g, cols].bitcast(FP8X4), scales=v_scales[:, g, cols], in_=v_grouped[:])

        def regroup_wo(engine_copy, wo_grouped, wo_raw, dh):
            engine_copy(
                out=wo_grouped[:, dh, :].rearrange("p (c i t) -> p c t i", i=4, t=PACK),
                in_=wo_raw[:, :, dh * BANK : (dh + 1) * BANK].rearrange("p t (c i) -> p c t i", i=4),
            )

        def quantise_wo(G, wo_grouped):
            nc.vector.quantize_mx(
                out=wo_codes[:, G, :].bitcast(FP8X4),
                scales=wo_scales[:, G, :],
                in_=wo_grouped[:].rearrange("p h w -> p (h w)"),
            )

        def transpose_u(c, u_raw):
            uT = stage.tile([P, UV_PASSES, P * 2], F32, tag="uT", bufs=5, name="uT")
            words = u_raw[:].bitcast(F32)
            for pair in range(PAIRS):
                bank = psum.tile([P, 2, 2, P], F32, tag="bank", bufs=2, name="u_bank")
                for i in range(2):
                    for h in range(2):
                        first = ((2 * pair + i) * 2 + h) * P
                        nc.tensor.transpose(bank[:, i, h, :], words[:, first : first + P], ident_f32[:])
                nc.scalar.copy(
                    out=uT[:, 2 * pair : 2 * pair + 2, :].rearrange("p i (n h) -> p i n h", h=2),
                    in_=bank[:].rearrange("p i h n -> p i n h"),
                )
            return uT

        def values_passes(c, pair):
            banks = []
            for i in range(2):
                G = 2 * pair + i
                bank = psum.tile([P, PACK, P], F32, tag="wide", bufs=6, name="av_bank")
                for j in range(PACK):
                    h, e = divmod(j, 2)
                    first = (G // 2) * 2 * K_PASS + e * K_PASS + (G % 2) * 2 * P + h * P
                    e_cols = slice(first, first + P)
                    for g in range(KEY_PASSES):
                        n_cols = slice(g * P, (g + 1) * P)
                        nc.tensor.matmul_mx(
                            out=bank[:, j, :],
                            lhsT=v_codes[:, g, e_cols].bitcast(FP8X4),
                            lhsT_scale=v_scales[:, g, e_cols],
                            rhs=at_codes[:, c, n_cols].bitcast(FP8X4),
                            rhs_scale=at_scales[:, c, n_cols],
                            start=(g == 0),
                            stop=(g == KEY_PASSES - 1),
                        )
                banks.append(bank)
            return banks

        def gate(uT, pair, banks, g_grouped):
            for i in range(2):
                G = 2 * pair + i
                nc.vector.tensor_tensor(
                    out=g_grouped[:, G, :].rearrange("p (n j) -> p n j", j=PACK),
                    in0=banks[i][:].rearrange("p j n -> p n j"),
                    in1=uT[:, G, :].bitcast(BF16).rearrange("p (n j) -> p n j", j=PACK),
                    op=ALU.mult,
                )

        def quantise_gated(g_grouped, g_codes, g_scales, first, passes):
            cols = slice(first * P, (first + passes) * P)
            nc.vector.quantize_mx(
                out=g_codes[:, cols].bitcast(FP8X4),
                scales=g_scales[:, cols],
                in_=g_grouped[:, first : first + passes, :].rearrange("p i w -> p (i w)"),
            )

        def output_passes(g_codes, g_scales):
            banks = []
            for dh in range(DIM_HALVES):
                bank = psum.tile([P, BANK], F32, tag="wide", bufs=6, name="o_bank")
                d_cols = slice(dh * BANK, (dh + 1) * BANK)
                for G in range(UV_PASSES):
                    n_cols = slice(G * P, (G + 1) * P)
                    nc.tensor.matmul_mx(
                        out=bank[:],
                        lhsT=g_codes[:, n_cols].bitcast(FP8X4),
                        lhsT_scale=g_scales[:, n_cols],
                        rhs=wo_codes[:, G, d_cols].bitcast(FP8X4),
                        rhs_scale=wo_scales[:, G, d_cols],
                        start=(G == 0),
                        stop=(G == UV_PASSES - 1),
                    )
                banks.append(bank)
            return banks

        def residual_and_bias(c, hid):
            o = stage.tile([P, DIM], F32, tag="o", bufs=4, name="o")
            for dh in range(DIM_HALVES):
                d_cols = slice(dh * BANK, (dh + 1) * BANK)
                nc.gpsimd.tensor_tensor(out=o[:, d_cols], in0=hid[:, c % (TILES // 2), d_cols], in1=bo_all[:, d_cols], op=ALU.add)
            return o

        def add_output(o, banks):
            for dh in range(DIM_HALVES):
                d_cols = slice(dh * BANK, (dh + 1) * BANK)
                nc.vector.tensor_tensor(out=o[:, d_cols], in0=banks[dh][:], in1=o[:, d_cols], op=ALU.add)

        def sumsq(o):
            sum_sq = small.tile([P, 1], F32, tag="sum_sq", name="sum_sq")
            inv_rms = small.tile([P, 1], F32, tag="inv_rms", name="inv_rms")
            nc.scalar.activation(out=squares[:], in_=o[:], func=ACT.Square, accum_out=sum_sq[:])
            nc.scalar.activation(out=inv_rms[:], in_=sum_sq[:], func=ACT.Abs_reciprocal_sqrt, scale=1.0 / DIM, bias=eps[:])
            return inv_rms
        def scale_store(c, o, inv_rms):
            nc.scalar.activation(out=o[:], in_=o[:], func=ACT.Copy, scale=inv_rms[:])
            nc.sync.dma_start(out=out_view[c], in_=o[:])

        nc.gpsimd.memset(bo_row[:], 0.0)
        nc.gpsimd.memset(ones[:], 1.0)
        nc.sync.dma_start(out=k_sb[:], in_=k_view)
        v_tiles = {(0, 0): [load_v(0, K_PASS, 0)]}
        nc.sync.dma_start(out=q_sb[:], in_=q_view)
        v_tiles[0, 0].append(load_v(K_PASS, K_PASS, 0))
        v_tiles[0, 1] = [load_v(i * K_PASS, K_PASS, 1) for i in range(2)]
        u_tiles = {0: load_u(0)}
        for g in range(KEY_PASSES):
            v_tiles[1, g] = [load_v(2 * K_PASS, 2 * K_PASS, g)]
            u_tiles[g + 1] = load_u(g + 1)
        u_tiles[3] = load_u(3)
        nc.sync.dma_start(out=bo_row[0:1, :], in_=bo.rearrange("(r d) -> r d", r=1))
        wo_tiles = {G: load_wo(G) for G in range(2)}

        make_identity(nc, ident_bf[:])
        make_identity(nc, ident_f32[:])
        nc.vector.memset(eps[:], NORM_EPS)
        nc.vector.memset(warm[:], 1.0)
        nc.scalar.activation(out=warm[:], in_=warm[:], func=ACT.Abs_reciprocal_sqrt)

        for g in range(KEY_PASSES):
            bank = psum.tile([P, PACK, P], BF16, tag="bank", bufs=2, name="k_bank")
            for t in range(PACK):
                nc.tensor.transpose(bank[:, t, :], k_sb[:, g, t * KEY : (t + 1) * KEY], ident_bf[:])
            nc.scalar.copy(out=kT[:, g, :, :], in_=bank[:])
        for half in range(2):
            tiles = TILES // 2
            bank = psum.tile([P, tiles, P], BF16, tag="bank", bufs=2, name="q_bank")
            for cl in range(tiles):
                nc.tensor.transpose(bank[:, cl, :], q_sb[:, half * tiles + cl, :], ident_bf[:])
            nc.scalar.copy(out=qT[:, half * tiles : (half + 1) * tiles, :], in_=bank[:])

        uT = {}
        at_pair = {}

        def prepare_tile(c):
            if c % 2 == 0:
                at_pair[0] = stage.tile([P, 2, KEY_PASSES * BANK], BF16, tag="at_grouped", bufs=2, name="at_grouped", align_bytes=64)
            attention_weights(c, at_pair[0])
            uT[c] = transpose_u(c, u_tiles[c])
            if c + UV_PASSES < TILES:
                u_tiles[c + UV_PASSES] = load_u(c + UV_PASSES)
            if c % 2 == 1:
                quantise_attention_weights(c // 2, at_pair[0])

        def prepare_wo(G):
            wo_grouped = stage.tile([P, DIM_HALVES, PACK * BANK], BF16, tag="wo_grouped", bufs=2, name="wo_grouped", align_bytes=64)
            regroup_wo(nc.vector.tensor_copy, wo_grouped, wo_tiles[G], 0)
            regroup_wo(nc.scalar.copy, wo_grouped, wo_tiles[G], 1)
            quantise_wo(G, wo_grouped)
            if G + 2 < UV_PASSES:
                wo_tiles[G + 2] = load_wo(G + 2)

        with tc.manual_schedule(engines={mybir.EngineType.PE}):
            v_parts = []
            for G in range(UV_PASSES):
                v_parts.append(regroup_v(v_tiles[divmod(G, KEY_PASSES)]))
                prepare_tile(G)
                for i in range(max(G - 1, 0), G if G < UV_PASSES - 1 else UV_PASSES):
                    quantise_v(*divmod(i, KEY_PASSES), v_parts[i])
                if G >= 2:
                    prepare_wo(G - 2)
            first_banks = values_passes(0, 0)

        hid_tiles = {part: load_hidden(part) for part in range(2)}

        for dh in range(DIM_HALVES):
            d_cols = slice(dh * BANK, (dh + 1) * BANK)
            bank = psum.tile([P, BANK], F32, tag="bank", bufs=2, name="bo_bank")
            nc.tensor.matmul(out=bank[:], lhsT=ones[:], rhs=bo_row[:, d_cols], start=True, stop=True)
            nc.scalar.copy(out=bo_all[:, d_cols], in_=bank[:])

        def finish_tile(c, o):
            banks = output_passes(*g_mx[c])
            add_output(o, banks)
            scale_store(c, o, sumsq(o))

        def finish_tile_by_halves(c, o, banks):
            sums = small.tile([P, DIM_HALVES], F32, tag="sums", name="sums")
            for dh in range(DIM_HALVES):
                d_cols = slice(dh * BANK, (dh + 1) * BANK)
                nc.vector.tensor_tensor(out=o[:, d_cols], in0=banks[dh][:], in1=o[:, d_cols], op=ALU.add)
                nc.scalar.activation(out=squares[:, d_cols], in_=o[:, d_cols], func=ACT.Square, accum_out=sums[:, dh : dh + 1])
            first_mean = small.tile([P, 1], F32, tag="first_mean", name="first_mean")
            inv_rms = small.tile([P, 1], F32, tag="inv_rms", name="inv_rms")
            nc.vector.tensor_scalar(
                out=first_mean[:], in0=sums[:, 0:1], scalar1=1.0 / DIM, scalar2=NORM_EPS, op0=ALU.mult, op1=ALU.add
            )
            nc.scalar.activation(
                out=inv_rms[:], in_=sums[:, 1:2], func=ACT.Abs_reciprocal_sqrt, scale=1.0 / DIM, bias=first_mean[:]
            )
            split = 3 * DIM // 8 if c == TILES - 1 else 0
            nc.vector.tensor_scalar(out=o[:, split:], in0=o[:, split:], scalar1=inv_rms[:], scalar2=None, op0=ALU.mult)
            nc.sync.dma_start(out=out_view[c][:, split:], in_=o[:, split:])
            if split > 0:
                nc.scalar.activation(out=o[:, :split], in_=o[:, :split], func=ACT.Copy, scale=inv_rms[:])
                nc.sync.dma_start(out=out_view[c][:, :split], in_=o[:, :split])

        o_tiles = {}
        g_mx = {}

        def next_residual(c):
            o_tiles[c] = residual_and_bias(c, hid_tiles[c // (TILES // 2)])

        next_residual(0)
        for c in range(TILES):
            banks = first_banks if c == 0 else values_passes(c, 0)
            g_grouped = stage.tile([P, UV_PASSES, BANK], BF16, tag="g_grouped", bufs=3, name="g_grouped", align_bytes=64)
            gate(uT[c], 0, banks, g_grouped)
            banks = values_passes(c, 1)
            if c + 1 < TILES:
                next_residual(c + 1)
            g_codes = stage.tile([P, UV_PASSES * P], U32, tag="g_codes", bufs=3, name="g_codes", align_bytes=64)
            g_scales = stage.tile([P, UV_PASSES * P], U8, tag="g_scales", bufs=3, name="g_scales", align_bytes=64)
            parts = PAIRS if c == TILES - 1 else 1
            if parts == PAIRS:
                quantise_gated(g_grouped, g_codes, g_scales, 0, 2)
            gate(uT[c], 1, banks, g_grouped)
            first = UV_PASSES - UV_PASSES // parts
            quantise_gated(g_grouped, g_codes, g_scales, first, UV_PASSES - first)
            g_mx[c] = (g_codes, g_scales)
            if c < 2:
                prepare_wo(c + 2)
            if c + AHEAD < TILES:
                prepare_tile(c + AHEAD)
            if 0 < c < TILES - 1:
                finish_tile(c - 1, o_tiles[c - 1])
        for c in range(TILES - 2, TILES):
            finish_tile_by_halves(c, o_tiles[c], output_passes(*g_mx[c]))
